import numpy as np
import ml_dtypes


def mxq(x, axis, fmt="e4m3"):
    dtype, down = {"e4m3": (ml_dtypes.float8_e4m3fn, 7), "e5m2": (ml_dtypes.float8_e5m2, 14)}[fmt]
    v = np.moveaxis(np.asarray(x, np.float32).astype(ml_dtypes.bfloat16).astype(np.float64), axis, -1)
    blocks = v.reshape(v.shape[:-1] + (-1, 32))
    amax = np.abs(blocks).max(-1, keepdims=True)
    byte = np.maximum(np.where(amax > 0, np.frexp(amax)[1] - 1 + 127, 0) - down, 1)
    scale = np.exp2(byte - 127.0)
    codes = (blocks / scale).astype(np.float32).astype(dtype).astype(np.float64)
    return np.moveaxis((codes * scale).reshape(v.shape), -1, axis)


WIDE = False


def mx_kscale(k):
    if not WIDE:
        return np.ones(k)
    levels = np.array([10, -10, 5, -5, 0])
    a = np.random.permutation(np.resize(levels, k // 512 * 4)).reshape(k // 512, 4)
    idx = np.arange(k)
    return np.exp2(a[idx // 512, idx % 128 // 32])


BF16 = ml_dtypes.bfloat16


def bf(x):
    return np.asarray(x, np.float32).astype(BF16)


def f64(x):
    return np.asarray(x).astype(np.float64)


N, M, MOL, PROT, F, D = 256, 512, 768, 1280, 8192, 512
EPS = 1e-8


def l2_normalise(v):
    return v / np.maximum(np.sqrt((v * v).sum(-1, keepdims=True)), EPS)


def setup_inputs():
    s, t = mx_kscale(F), mx_kscale(F)
    return {
        "h_mol": bf(np.maximum(np.random.standard_normal((N, F)), 0.0) * s),
        "h_prot": bf(np.maximum(np.random.standard_normal((M, F)), 0.0) * t),
        "Wm2": bf(np.random.standard_normal((D, F)) / np.sqrt(F) / s),
        "bm2": bf(np.random.standard_normal(D) * 0.2),
        "Wp2": bf(np.random.standard_normal((D, F)) / np.sqrt(F) / t),
        "bp2": bf(np.random.standard_normal(D) * 0.2),
        "temperature": bf(0.1 * (1.0 + 0.1 * np.random.standard_normal(1))),
    }


def reference(h_mol, h_prot, Wm2, bm2, Wp2, bp2, temperature):
    mp = (mxq(f64(h_mol), 1, "e4m3") @ mxq(f64(Wm2), 1, "e4m3").T) + f64(bm2)
    pp = (mxq(f64(h_prot), 1, "e4m3") @ mxq(f64(Wp2), 1, "e4m3").T) + f64(bp2)
    mn = l2_normalise(mp)
    pn = l2_normalise(pp)
    distance = mxq(pn, 1, "e4m3") @ mxq(mn, 1, "e4m3").T
    return distance / f64(temperature)

@@ -1,0 +1,265 @@
+from contextlib import ExitStack
+
+import concourse.mybir as mybir
+from concourse.masks import make_identity
+
+F32 = mybir.dt.float32
+BF16 = mybir.dt.bfloat16
+U32 = mybir.dt.uint32
+U8 = mybir.dt.uint8
+FP8X4 = mybir.dt.float8_e4m3fn_x4
+ALU = mybir.AluOpType
+ACT = mybir.ActivationFunctionType
+
+N_MOL, M_PROT, F, D = 256, 512, 8192, 512
+EPS = 1e-8
+FLOPS = 2 * F * D * (N_MOL + M_PROT) + 2 * M_PROT * N_MOL * D
+
+P = 128
+PACK = 4
+K_PASS = P * PACK
+PASSES = F // K_PASS
+WORDS = K_PASS // 2
+W_TILES = D // P
+CHUNK = 1024
+PASSES_PER_CHUNK = CHUNK // K_PASS
+CHUNKS = F // CHUNK
+RAW_BUFS = 6
+LAG = 2
+GROUP = 2 * P
+TEMP_COLS = 32
+
+
+def tile_coembedding_pa_k_kernel(tc, h_mol, h_prot, Wm2, bm2, Wp2, bp2, temperature, out):
+    nc = tc.nc
+    with ExitStack() as ctx:
+        const = ctx.enter_context(tc.tile_pool(name="const", bufs=1))
+        raw_pool = ctx.enter_context(tc.tile_pool(name="raw", bufs=RAW_BUFS))
+        grouped_pool = ctx.enter_context(tc.tile_pool(name="grouped", bufs=3))
+        codes_pool = ctx.enter_context(tc.tile_pool(name="codes", bufs=3))
+        finish_pool = ctx.enter_context(tc.tile_pool(name="finish", bufs=4))
+        acc_psum = ctx.enter_context(tc.psum_pool(name="acc_psum", bufs=4))
+        turn_psum = ctx.enter_context(tc.psum_pool(name="turn_psum", bufs=4))
+        ctx.enter_context(tc.manual_schedule())
+
+        streams = (
+            {"h": h_prot, "w": Wp2, "h_tiles": M_PROT // P},
+            {"h": h_mol, "w": Wm2, "h_tiles": N_MOL // P},
+        )
+        n_jobs = len(streams) * PASSES
+
+        raw = {}
+
+        def load_chunk(chunk):
+            stream = streams[chunk // CHUNKS]
+            k_first = (chunk % CHUNKS) * CHUNK
+            w_raw = raw_pool.tile([P, W_TILES, CHUNK], BF16, tag="w_raw")
+            h_raw = raw_pool.tile([P, stream["h_tiles"], CHUNK], BF16, tag="h_raw")
+            width = K_PASS if chunk == 0 else CHUNK
+            for first in range(0, CHUNK, width):
+                for target, matrix in ((w_raw, stream["w"]), (h_raw, stream["h"])):
+                    nc.sync.dma_start(
+                        out=target[:, :, first : first + width],
+                        in_=matrix.rearrange("(t p) k -> p t k", p=P)[
+                            :, :, k_first + first : k_first + first + width
+                        ],
+                    )
+            raw[chunk] = (w_raw, h_raw)
+
+        for chunk in range(RAW_BUFS):
+            load_chunk(chunk)
+
+        ident_f32 = const.tile([P, P], F32)
+        make_identity(nc, ident_f32[:])
+        ident_bf16 = const.tile([P, P], BF16)
+        make_identity(nc, ident_bf16[:])
+        ones = const.tile([P, P], BF16)
+        nc.vector.memset(ones[:], 1.0)
+        rows = const.tile([P, 2 * D + TEMP_COLS], BF16)
+        nc.vector.memset(rows[:], 0.0)
+        nc.scalar.dma_start(out=rows[0:1, 0:D], in_=bp2.rearrange("(o d) -> o d", o=1))
+        nc.scalar.dma_start(out=rows[0:1, D : 2 * D], in_=bm2.rearrange("(o d) -> o d", o=1))
+        nc.scalar.dma_start(out=rows[0:1, 2 * D : 2 * D + 1], in_=temperature.rearrange("(o d) -> o d", o=1))
+        one = const.tile([P, 1], F32)
+        nc.vector.memset(one[:], 1.0)
+        root_of_one = const.tile([P, 1], F32)
+        nc.scalar.sqrt(out=root_of_one[:], in_=one[:])
+
+        bias_prot = const.tile([P, D], F32)
+        bias_mol = const.tile([P, D], F32)
+        inv_temperature = const.tile([P, 1], F32)
+
+        def spread_constants():
+            for bias, first in ((bias_prot, 0), (bias_mol, D)):
+                spread = turn_psum.tile([P, D], F32, tag="turn")
+                nc.tensor.matmul(out=spread[:], lhsT=ones[:], rhs=rows[:, first : first + D], start=True, stop=True)
+                nc.vector.tensor_copy(out=bias[:], in_=spread[:])
+            spread_t = turn_psum.tile([P, TEMP_COLS], F32, tag="turn")
+            nc.tensor.matmul(out=spread_t[:], lhsT=ones[:], rhs=rows[:, 2 * D :], start=True, stop=True)
+            nc.vector.reciprocal(out=inv_temperature[:], in_=spread_t[:, 0:1])
+
+        grouped = {}
+        codes = {}
+        acc = {}
+
+        def transpose_job(job):
+            stream = streams[job // PASSES]
+            w_raw, h_raw = raw[job // PASSES_PER_CHUNK]
+            word_first = (job % PASSES_PER_CHUNK) * WORDS
+            w_grouped = grouped_pool.tile([P, D * PACK], BF16, tag="w_grouped", align_bytes=64)
+            h_grouped = grouped_pool.tile([P, stream["h_tiles"] * P * PACK], BF16, tag="h_grouped", align_bytes=64)
+            banks = [(w_raw, w_grouped, pair) for pair in range(W_TILES // 2)]
+            banks += [(h_raw, h_grouped, pair) for pair in range(stream["h_tiles"] // 2)]
+            for index, (source, target, pair) in enumerate(banks):
+                words = source[:].bitcast(F32)
+                bank = turn_psum.tile([P, 4, P], F32, tag="turn")
+                for a in range(2):
+                    for u in range(2):
+                        nc.tensor.transpose(
+                            out=bank[:, 2 * a + u, :],
+                            in_=words[:, 2 * pair + a, word_first + u * P : word_first + (u + 1) * P],
+                            identity=ident_f32[:],
+                        )
+                turned = bank[:].rearrange("p (a u) r -> p a r u", u=2)
+                side_by_side = target[:].bitcast(F32).rearrange("p (t r u) -> p t r u", r=P, u=2)
+                side_by_side = side_by_side[:, 2 * pair : 2 * pair + 2]
+                if index == len(banks) - 1:
+                    nc.vector.tensor_copy(out=side_by_side, in_=turned)
+                else:
+                    nc.scalar.copy(out=side_by_side, in_=turned)
+            grouped[job] = (w_grouped, h_grouped)
+
+        def quantise_job(job):
+            h_cols = streams[job // PASSES]["h_tiles"] * P
+            w_grouped, h_grouped = grouped[job]
+            w_words = codes_pool.tile([P, D], U32, tag="w_words", align_bytes=64)
+            w_scales = codes_pool.tile([P, D], U8, tag="w_scales", align_bytes=64)
+            h_words = codes_pool.tile([P, h_cols], U32, tag="h_words", align_bytes=64)
+            h_scales = codes_pool.tile([P, h_cols], U8, tag="h_scales", align_bytes=64)
+            nc.vector.quantize_mx(out=w_words[:].bitcast(FP8X4), scales=w_scales[:], in_=w_grouped[:])
+            nc.vector.quantize_mx(out=h_words[:].bitcast(FP8X4), scales=h_scales[:], in_=h_grouped[:])
+            codes[job] = (w_words, w_scales, h_words, h_scales)
+
+        def multiply_job(job):
+            number, g = divmod(job, PASSES)
+            if g == 0:
+                acc[number] = []
+                for i in range(streams[number]["h_tiles"]):
+                    acc_tile = acc_psum.tile([P, D], F32, tag="acc")
+                    acc[number].append(acc_tile)
+            w_words, w_scales, h_words, h_scales = codes[job]
+            for i, acc_tile in enumerate(acc[number]):
+                nc.tensor.matmul_mx(
+                    out=acc_tile[:],
+                    lhsT=h_words[:, i * P : (i + 1) * P].bitcast(FP8X4),
+                    lhsT_scale=h_scales[:, i * P : (i + 1) * P],
+                    rhs=w_words[:].bitcast(FP8X4),
+                    rhs_scale=w_scales[:],
+                    start=(g == 0),
+                    stop=(g == PASSES - 1),
+                )
+
+        prot_words = const.tile([P, M_PROT], U32, align_bytes=64)
+        prot_scales = const.tile([P, M_PROT], U8, align_bytes=64)
+        mol_words = const.tile([P, N_MOL], U32, align_bytes=64)
+        mol_scales = const.tile([P, N_MOL], U8, align_bytes=64)
+        groups = (
+            {"stream": 0, "first": 0, "bias": bias_prot, "words": prot_words, "scales": prot_scales},
+            {"stream": 0, "first": 2, "bias": bias_prot, "words": prot_words, "scales": prot_scales},
+            {"stream": 1, "first": 0, "bias": bias_mol, "words": mol_words, "scales": mol_scales},
+        )
+
+        def add_bias_and_square(group):
+            group["v"] = []
+            sum_sq = finish_pool.tile([P, 2], F32, tag="sum_sq")
+            for a in range(2):
+                v = finish_pool.tile([P, D], F32, tag="v")
+                nc.vector.tensor_tensor(
+                    out=v[:], in0=acc[group["stream"]][group["first"] + a][:], in1=group["bias"][:], op=ALU.add
+                )
+                group["v"].append(v)
+            for a in range(2):
+                squares = finish_pool.tile([P, D], BF16, tag="squares")
+                nc.scalar.activation(
+                    out=squares[:], in_=group["v"][a][:], func=ACT.Square, accum_out=sum_sq[:, a : a + 1]
+                )
+            group["sum_sq"] = sum_sq
+
+        def clamp_and_root(group):
+            clamped = finish_pool.tile([P, 2], F32, tag="clamped")
+            nc.vector.tensor_scalar_max(out=clamped[:], in0=group["sum_sq"][:], scalar1=EPS * EPS)
+            norm = finish_pool.tile([P, 2], F32, tag="norm")
+            nc.scalar.sqrt(out=norm[:], in_=clamped[:])
+            group["norm"] = norm
+
+        def scale_to_unit(group):
+            inv_norm = finish_pool.tile([P, 2], F32, tag="inv_norm")
+            nc.vector.reciprocal(out=inv_norm[:], in_=group["norm"][:])
+            group["unit"] = []
+            for a in range(2):
+                unit = finish_pool.tile([P, D], BF16, tag="unit")
+                nc.vector.tensor_scalar_mul(out=unit[:], in0=group["v"][a][:], scalar1=inv_norm[:, a : a + 1])
+                group["unit"].append(unit)
+
+        def transpose_unit(group):
+            unit_grouped = finish_pool.tile([P, GROUP * PACK], BF16, tag="unit_grouped", align_bytes=64)
+            for a in range(2):
+                bank = turn_psum.tile([P, PACK, P], BF16, tag="turn")
+                for t in range(PACK):
+                    nc.tensor.transpose(
+                        out=bank[:, t, :], in_=group["unit"][a][:, t * P : (t + 1) * P], identity=ident_bf16[:]
+                    )
+                turned = bank[:].rearrange("p t r -> p r t")
+                side_by_side = unit_grouped[:, a * K_PASS : (a + 1) * K_PASS].rearrange("p (r t) -> p r t", t=PACK)
+                if a == 0:
+                    nc.scalar.copy(out=side_by_side, in_=turned)
+                else:
+                    nc.vector.tensor_copy(out=side_by_side, in_=turned)
+            group["unit_grouped"] = unit_grouped
+
+        def quantise_unit(group):
+            cols = slice(group["first"] * P, group["first"] * P + GROUP)
+            nc.vector.quantize_mx(
+                out=group["words"][:, cols].bitcast(FP8X4),
+                scales=group["scales"][:, cols],
+                in_=group["unit_grouped"][:],
+            )
+
+        finish_stages = (add_bias_and_square, clamp_and_root, scale_to_unit, transpose_unit, quantise_unit)
+
+        protein_closes = PASSES - 1 + LAG
+        for i in range(n_jobs + LAG):
+            if 1 <= i <= n_jobs:
+                quantise_job(i - 1)
+            if i < n_jobs:
+                transpose_job(i)
+                next_chunk = i // PASSES_PER_CHUNK + RAW_BUFS
+                if (i + 1) % PASSES_PER_CHUNK == 0 and next_chunk < len(streams) * CHUNKS:
+                    load_chunk(next_chunk)
+            if i == 0:
+                spread_constants()
+            if i >= LAG:
+                multiply_job(i - LAG)
+            step = i - protein_closes
+            if 0 <= step < 2 * len(finish_stages):
+                finish_stages[step % len(finish_stages)](groups[step // len(finish_stages)])
+        for stage in finish_stages:
+            stage(groups[2])
+
+        for i in range(M_PROT // P):
+            distance = acc_psum.tile([P, N_MOL], F32, tag="acc")
+            nc.tensor.matmul_mx(
+                out=distance[:],
+                lhsT=prot_words[:, i * P : (i + 1) * P].bitcast(FP8X4),
+                lhsT_scale=prot_scales[:, i * P : (i + 1) * P],
+                rhs=mol_words[:].bitcast(FP8X4),
+                rhs_scale=mol_scales[:],
+                start=True,
+                stop=True,
+            )
+            result = finish_pool.tile([P, N_MOL], F32, tag="result")
+            if i % 2 == 0:
+                nc.scalar.activation(out=result[:], in_=distance[:], func=ACT.Copy, scale=inv_temperature[:, 0:1])
+            else:
+                nc.vector.tensor_scalar_mul(out=result[:], in0=distance[:], scalar1=inv_temperature[:, 0:1])
+            nc.sync.dma_start(out=out[i * P : (i + 1) * P, :], in_=result[:])

@@ -40,7 +40,6 @@ def tile_coembedding_pa_k_kernel(tc, h_mol, h_prot, Wm2, bm2, Wp2, bp2, temperat
         finish_pool = ctx.enter_context(tc.tile_pool(name="finish", bufs=4))
         acc_psum = ctx.enter_context(tc.psum_pool(name="acc_psum", bufs=4))
         turn_psum = ctx.enter_context(tc.psum_pool(name="turn_psum", bufs=4))
-        ctx.enter_context(tc.manual_schedule())
 
         streams = (
             {"h": h_prot, "w": Wp2, "h_tiles": M_PROT // P},

@@ -21,11 +21,10 @@ K_PASS = P * PACK
 PASSES = F // K_PASS
 WORDS = K_PASS // 2
 W_TILES = D // P
-CHUNK = 1024
-PASSES_PER_CHUNK = CHUNK // K_PASS
-CHUNKS = F // CHUNK
-RAW_BUFS = 6
-LAG = 2
+ROUND = 2
+ROUND_K = ROUND * K_PASS
+ROUNDS = PASSES // ROUND
+RAW_BUFS = 48
 GROUP = 2 * P
 TEMP_COLS = 32
 
@@ -35,38 +34,45 @@ def tile_coembedding_pa_k_kernel(tc, h_mol, h_prot, Wm2, bm2, Wp2, bp2, temperat
     with ExitStack() as ctx:
         const = ctx.enter_context(tc.tile_pool(name="const", bufs=1))
         raw_pool = ctx.enter_context(tc.tile_pool(name="raw", bufs=RAW_BUFS))
-        grouped_pool = ctx.enter_context(tc.tile_pool(name="grouped", bufs=3))
-        codes_pool = ctx.enter_context(tc.tile_pool(name="codes", bufs=3))
+        grouped_pool = ctx.enter_context(tc.tile_pool(name="grouped", bufs=2))
+        codes_pool = ctx.enter_context(tc.tile_pool(name="codes", bufs=2))
         finish_pool = ctx.enter_context(tc.tile_pool(name="finish", bufs=4))
-        acc_psum = ctx.enter_context(tc.psum_pool(name="acc_psum", bufs=4))
-        turn_psum = ctx.enter_context(tc.psum_pool(name="turn_psum", bufs=4))
+        psum = ctx.enter_context(tc.psum_pool(name="psum", bufs=1))
 
         streams = (
             {"h": h_prot, "w": Wp2, "h_tiles": M_PROT // P},
             {"h": h_mol, "w": Wm2, "h_tiles": N_MOL // P},
         )
-        n_jobs = len(streams) * PASSES
+        n_rounds = len(streams) * ROUNDS
+
+        def psum_tile(bank, shape, dtype):
+            bank_tile = psum.tile(shape, dtype, tag="bank%d" % bank)
+            return bank_tile
+
+        turn_banks = [4, 5, 6, 7]
+        turned_so_far = []
+
+        def turn_tile(shape, dtype):
+            bank = turn_banks[len(turned_so_far) % len(turn_banks)]
+            turned_so_far.append(bank)
+            return psum_tile(bank, shape, dtype)
 
         raw = {}
 
-        def load_chunk(chunk):
-            stream = streams[chunk // CHUNKS]
-            k_first = (chunk % CHUNKS) * CHUNK
-            w_raw = raw_pool.tile([P, W_TILES, CHUNK], BF16, tag="w_raw")
-            h_raw = raw_pool.tile([P, stream["h_tiles"], CHUNK], BF16, tag="h_raw")
-            width = K_PASS if chunk == 0 else CHUNK
-            for first in range(0, CHUNK, width):
-                for target, matrix in ((w_raw, stream["w"]), (h_raw, stream["h"])):
+        def load_round(r):
+            stream = streams[r // ROUNDS]
+            k_first = (r % ROUNDS) * ROUND_K
+            for name, matrix, tiles in (("w", stream["w"], W_TILES), ("h", stream["h"], stream["h_tiles"])):
+                for t in range(tiles):
+                    rows_tile = raw_pool.tile([P, ROUND_K], BF16, tag="rows")
                     nc.sync.dma_start(
-                        out=target[:, :, first : first + width],
-                        in_=matrix.rearrange("(t p) k -> p t k", p=P)[
-                            :, :, k_first + first : k_first + first + width
-                        ],
+                        out=rows_tile[:], in_=matrix[t * P : (t + 1) * P, k_first : k_first + ROUND_K]
                     )
-            raw[chunk] = (w_raw, h_raw)
+                    raw[(r, name, t)] = rows_tile
 
-        for chunk in range(RAW_BUFS):
-            load_chunk(chunk)
+        load_ahead = RAW_BUFS // (W_TILES + M_PROT // P)
+        for r in range(load_ahead):
+            load_round(r)
 
         ident_f32 = const.tile([P, P], F32)
         make_identity(nc, ident_f32[:])
@@ -90,10 +96,10 @@ def tile_coembedding_pa_k_kernel(tc, h_mol, h_prot, Wm2, bm2, Wp2, bp2, temperat
 
         def spread_constants():
             for bias, first in ((bias_prot, 0), (bias_mol, D)):
-                spread = turn_psum.tile([P, D], F32, tag="turn")
+                spread = turn_tile([P, D], F32)
                 nc.tensor.matmul(out=spread[:], lhsT=ones[:], rhs=rows[:, first : first + D], start=True, stop=True)
                 nc.vector.tensor_copy(out=bias[:], in_=spread[:])
-            spread_t = turn_psum.tile([P, TEMP_COLS], F32, tag="turn")
+            spread_t = turn_tile([P, TEMP_COLS], F32)
             nc.tensor.matmul(out=spread_t[:], lhsT=ones[:], rhs=rows[:, 2 * D :], start=True, stop=True)
             nc.vector.reciprocal(out=inv_temperature[:], in_=spread_t[:, 0:1])
 
@@ -101,62 +107,68 @@ def tile_coembedding_pa_k_kernel(tc, h_mol, h_prot, Wm2, bm2, Wp2, bp2, temperat
         codes = {}
         acc = {}
 
-        def transpose_job(job):
-            stream = streams[job // PASSES]
-            w_raw, h_raw = raw[job // PASSES_PER_CHUNK]
-            word_first = (job % PASSES_PER_CHUNK) * WORDS
-            w_grouped = grouped_pool.tile([P, D * PACK], BF16, tag="w_grouped", align_bytes=64)
-            h_grouped = grouped_pool.tile([P, stream["h_tiles"] * P * PACK], BF16, tag="h_grouped", align_bytes=64)
-            banks = [(w_raw, w_grouped, pair) for pair in range(W_TILES // 2)]
-            banks += [(h_raw, h_grouped, pair) for pair in range(stream["h_tiles"] // 2)]
-            for index, (source, target, pair) in enumerate(banks):
-                words = source[:].bitcast(F32)
-                bank = turn_psum.tile([P, 4, P], F32, tag="turn")
-                for a in range(2):
-                    for u in range(2):
-                        nc.tensor.transpose(
-                            out=bank[:, 2 * a + u, :],
-                            in_=words[:, 2 * pair + a, word_first + u * P : word_first + (u + 1) * P],
-                            identity=ident_f32[:],
-                        )
+        def transpose_round(r):
+            stream = streams[r // ROUNDS]
+            w_grouped = grouped_pool.tile([P, ROUND * D * PACK], BF16, tag="w_grouped", align_bytes=64)
+            h_grouped = grouped_pool.tile([P, ROUND * stream["h_tiles"] * P * PACK], BF16, tag="h_grouped", align_bytes=64)
+            row_tiles = [("w", t, w_grouped, W_TILES) for t in range(W_TILES)]
+            row_tiles += [("h", t, h_grouped, stream["h_tiles"]) for t in range(stream["h_tiles"])]
+            for index, (name, t, target, tiles) in enumerate(row_tiles):
+                words = raw[(r, name, t)][:].bitcast(F32)
+                bank = turn_tile([P, 2 * ROUND, P], F32)
+                for block in range(2 * ROUND):
+                    nc.tensor.transpose(
+                        out=bank[:, block, :], in_=words[:, block * P : (block + 1) * P], identity=ident_f32[:]
+                    )
                 turned = bank[:].rearrange("p (a u) r -> p a r u", u=2)
-                side_by_side = target[:].bitcast(F32).rearrange("p (t r u) -> p t r u", r=P, u=2)
-                side_by_side = side_by_side[:, 2 * pair : 2 * pair + 2]
-                if index == len(banks) - 1:
+                side_by_side = target[:].bitcast(F32).rearrange("p (a t r u) -> p a t r u", a=ROUND, t=tiles, u=2)
+                side_by_side = side_by_side[:, :, t]
+                if index in (2, 4, 6):
                     nc.vector.tensor_copy(out=side_by_side, in_=turned)
                 else:
                     nc.scalar.copy(out=side_by_side, in_=turned)
-            grouped[job] = (w_grouped, h_grouped)
+            grouped[r] = (w_grouped, h_grouped)
 
-        def quantise_job(job):
-            h_cols = streams[job // PASSES]["h_tiles"] * P
-            w_grouped, h_grouped = grouped[job]
-            w_words = codes_pool.tile([P, D], U32, tag="w_words", align_bytes=64)
-            w_scales = codes_pool.tile([P, D], U8, tag="w_scales", align_bytes=64)
-            h_words = codes_pool.tile([P, h_cols], U32, tag="h_words", align_bytes=64)
-            h_scales = codes_pool.tile([P, h_cols], U8, tag="h_scales", align_bytes=64)
-            nc.vector.quantize_mx(out=w_words[:].bitcast(FP8X4), scales=w_scales[:], in_=w_grouped[:])
-            nc.vector.quantize_mx(out=h_words[:].bitcast(FP8X4), scales=h_scales[:], in_=h_grouped[:])
-            codes[job] = (w_words, w_scales, h_words, h_scales)
+        def quantise_round(r):
+            h_cols = streams[r // ROUNDS]["h_tiles"] * P
+            w_grouped, h_grouped = grouped[r]
+            w_words = codes_pool.tile([P, ROUND * D], U32, tag="w_words", align_bytes=64)
+            w_scales = codes_pool.tile([P, ROUND * D], U8, tag="w_scales", align_bytes=64)
+            h_words = codes_pool.tile([P, ROUND * h_cols], U32, tag="h_words", align_bytes=64)
+            h_scales = codes_pool.tile([P, ROUND * h_cols], U8, tag="h_scales", align_bytes=64)
+            for a in range(ROUND):
+                for words, scales, source, cols in (
+                    (w_words, w_scales, w_grouped, D),
+                    (h_words, h_scales, h_grouped, h_cols),
+                ):
+                    nc.vector.quantize_mx(
+                        out=words[:, a * cols : (a + 1) * cols].bitcast(FP8X4),
+                        scales=scales[:, a * cols : (a + 1) * cols],
+                        in_=source[:, a * cols * PACK : (a + 1) * cols * PACK],
+                    )
+            codes[r] = (w_words, w_scales, h_words, h_scales)
 
-        def multiply_job(job):
-            number, g = divmod(job, PASSES)
-            if g == 0:
+        def multiply_round(r):
+            number = r // ROUNDS
+            h_cols = streams[number]["h_tiles"] * P
+            if r % ROUNDS == 0:
                 acc[number] = []
                 for i in range(streams[number]["h_tiles"]):
-                    acc_tile = acc_psum.tile([P, D], F32, tag="acc")
+                    acc_tile = psum_tile(i, [P, D], F32)
                     acc[number].append(acc_tile)
-            w_words, w_scales, h_words, h_scales = codes[job]
-            for i, acc_tile in enumerate(acc[number]):
-                nc.tensor.matmul_mx(
-                    out=acc_tile[:],
-                    lhsT=h_words[:, i * P : (i + 1) * P].bitcast(FP8X4),
-                    lhsT_scale=h_scales[:, i * P : (i + 1) * P],
-                    rhs=w_words[:].bitcast(FP8X4),
-                    rhs_scale=w_scales[:],
-                    start=(g == 0),
-                    stop=(g == PASSES - 1),
-                )
+            w_words, w_scales, h_words, h_scales = codes[r]
+            for a in range(ROUND):
+                for i, acc_tile in enumerate(acc[number]):
+                    h_first = a * h_cols + i * P
+                    nc.tensor.matmul_mx(
+                        out=acc_tile[:],
+                        lhsT=h_words[:, h_first : h_first + P].bitcast(FP8X4),
+                        lhsT_scale=h_scales[:, h_first : h_first + P],
+                        rhs=w_words[:, a * D : (a + 1) * D].bitcast(FP8X4),
+                        rhs_scale=w_scales[:, a * D : (a + 1) * D],
+                        start=(r % ROUNDS == 0 and a == 0),
+                        stop=(r % ROUNDS == ROUNDS - 1 and a == ROUND - 1),
+                    )
 
         prot_words = const.tile([P, M_PROT], U32, align_bytes=64)
         prot_scales = const.tile([P, M_PROT], U8, align_bytes=64)
@@ -203,7 +215,7 @@ def tile_coembedding_pa_k_kernel(tc, h_mol, h_prot, Wm2, bm2, Wp2, bp2, temperat
         def transpose_unit(group):
             unit_grouped = finish_pool.tile([P, GROUP * PACK], BF16, tag="unit_grouped", align_bytes=64)
             for a in range(2):
-                bank = turn_psum.tile([P, PACK, P], BF16, tag="turn")
+                bank = turn_tile([P, PACK, P], BF16)
                 for t in range(PACK):
                     nc.tensor.transpose(
                         out=bank[:, t, :], in_=group["unit"][a][:, t * P : (t + 1) * P], identity=ident_bf16[:]
@@ -226,27 +238,30 @@ def tile_coembedding_pa_k_kernel(tc, h_mol, h_prot, Wm2, bm2, Wp2, bp2, temperat
 
         finish_stages = (add_bias_and_square, clamp_and_root, scale_to_unit, transpose_unit, quantise_unit)
 
-        protein_closes = PASSES - 1 + LAG
-        for i in range(n_jobs + LAG):
-            if 1 <= i <= n_jobs:
-                quantise_job(i - 1)
-            if i < n_jobs:
-                transpose_job(i)
-                next_chunk = i // PASSES_PER_CHUNK + RAW_BUFS
-                if (i + 1) % PASSES_PER_CHUNK == 0 and next_chunk < len(streams) * CHUNKS:
-                    load_chunk(next_chunk)
+        for i in range(n_rounds + 1):
+            if i >= 1:
+                quantise_round(i - 1)
+            if i < n_rounds:
+                transpose_round(i)
+                if i + load_ahead < n_rounds:
+                    load_round(i + load_ahead)
             if i == 0:
                 spread_constants()
-            if i >= LAG:
-                multiply_job(i - LAG)
-            step = i - protein_closes
-            if 0 <= step < 2 * len(finish_stages):
-                finish_stages[step % len(finish_stages)](groups[step // len(finish_stages)])
+            if i >= 1:
+                multiply_round(i - 1)
+            if i == ROUNDS:
+                add_bias_and_square(groups[0])
+                add_bias_and_square(groups[1])
+                turn_banks.extend((2, 3))
+            step = i - ROUNDS - 1
+            if 0 <= step < 4:
+                for stage in (clamp_and_root, scale_to_unit) if step % 2 == 0 else (transpose_unit, quantise_unit):
+                    stage(groups[step // 2])
         for stage in finish_stages:
             stage(groups[2])
 
         for i in range(M_PROT // P):
-            distance = acc_psum.tile([P, N_MOL], F32, tag="acc")
+            distance = turn_tile([P, N_MOL], F32)
             nc.tensor.matmul_mx(
                 out=distance[:],
                 lhsT=prot_words[:, i * P : (i + 1) * P].bitcast(FP8X4),

@@ -25,7 +25,6 @@ ROUND = 2
 ROUND_K = ROUND * K_PASS
 ROUNDS = PASSES // ROUND
 RAW_BUFS = 48
-GROUP = 2 * P
 TEMP_COLS = 32
 
 
@@ -107,13 +106,16 @@ def tile_coembedding_pa_k_kernel(tc, h_mol, h_prot, Wm2, bm2, Wp2, bp2, temperat
         codes = {}
         acc = {}
 
-        def transpose_round(r):
+        def open_round(r):
             stream = streams[r // ROUNDS]
             w_grouped = grouped_pool.tile([P, ROUND * D * PACK], BF16, tag="w_grouped", align_bytes=64)
             h_grouped = grouped_pool.tile([P, ROUND * stream["h_tiles"] * P * PACK], BF16, tag="h_grouped", align_bytes=64)
-            row_tiles = [("w", t, w_grouped, W_TILES) for t in range(W_TILES)]
-            row_tiles += [("h", t, h_grouped, stream["h_tiles"]) for t in range(stream["h_tiles"])]
-            for index, (name, t, target, tiles) in enumerate(row_tiles):
+            grouped[r] = (w_grouped, h_grouped)
+
+        def transpose_operand(r, name):
+            tiles = W_TILES if name == "w" else streams[r // ROUNDS]["h_tiles"]
+            target = grouped[r][0 if name == "w" else 1]
+            for t in range(tiles):
                 words = raw[(r, name, t)][:].bitcast(F32)
                 bank = turn_tile([P, 2 * ROUND, P], F32)
                 for block in range(2 * ROUND):
@@ -123,11 +125,10 @@ def tile_coembedding_pa_k_kernel(tc, h_mol, h_prot, Wm2, bm2, Wp2, bp2, temperat
                 turned = bank[:].rearrange("p (a u) r -> p a r u", u=2)
                 side_by_side = target[:].bitcast(F32).rearrange("p (a t r u) -> p a t r u", a=ROUND, t=tiles, u=2)
                 side_by_side = side_by_side[:, :, t]
-                if index in (2, 4, 6):
+                if (name, t) in (("w", 2), ("h", 0), ("h", 2)):
                     nc.vector.tensor_copy(out=side_by_side, in_=turned)
                 else:
                     nc.scalar.copy(out=side_by_side, in_=turned)
-            grouped[r] = (w_grouped, h_grouped)
 
         def quantise_round(r):
             h_cols = streams[r // ROUNDS]["h_tiles"] * P
@@ -148,132 +149,144 @@ def tile_coembedding_pa_k_kernel(tc, h_mol, h_prot, Wm2, bm2, Wp2, bp2, temperat
                     )
             codes[r] = (w_words, w_scales, h_words, h_scales)
 
-        def multiply_round(r):
+        def multiply_tile(r, a, i):
             number = r // ROUNDS
             h_cols = streams[number]["h_tiles"] * P
-            if r % ROUNDS == 0:
-                acc[number] = []
-                for i in range(streams[number]["h_tiles"]):
-                    acc_tile = psum_tile(i, [P, D], F32)
-                    acc[number].append(acc_tile)
+            acc_tiles = acc.setdefault(number, [])
+            if i == len(acc_tiles):
+                acc_tile = psum_tile(i, [P, D], F32)
+                acc_tiles.append(acc_tile)
             w_words, w_scales, h_words, h_scales = codes[r]
-            for a in range(ROUND):
-                for i, acc_tile in enumerate(acc[number]):
-                    h_first = a * h_cols + i * P
-                    nc.tensor.matmul_mx(
-                        out=acc_tile[:],
-                        lhsT=h_words[:, h_first : h_first + P].bitcast(FP8X4),
-                        lhsT_scale=h_scales[:, h_first : h_first + P],
-                        rhs=w_words[:, a * D : (a + 1) * D].bitcast(FP8X4),
-                        rhs_scale=w_scales[:, a * D : (a + 1) * D],
-                        start=(r % ROUNDS == 0 and a == 0),
-                        stop=(r % ROUNDS == ROUNDS - 1 and a == ROUND - 1),
-                    )
+            h_first = a * h_cols + i * P
+            nc.tensor.matmul_mx(
+                out=acc_tiles[i][:],
+                lhsT=h_words[:, h_first : h_first + P].bitcast(FP8X4),
+                lhsT_scale=h_scales[:, h_first : h_first + P],
+                rhs=w_words[:, a * D : (a + 1) * D].bitcast(FP8X4),
+                rhs_scale=w_scales[:, a * D : (a + 1) * D],
+                start=(r % ROUNDS == 0 and a == 0),
+                stop=(r % ROUNDS == ROUNDS - 1 and a == ROUND - 1),
+            )
+
+        def multiply_pass(r, a):
+            for i in range(streams[r // ROUNDS]["h_tiles"]):
+                multiply_tile(r, a, i)
 
         prot_words = const.tile([P, M_PROT], U32, align_bytes=64)
         prot_scales = const.tile([P, M_PROT], U8, align_bytes=64)
         mol_words = const.tile([P, N_MOL], U32, align_bytes=64)
         mol_scales = const.tile([P, N_MOL], U8, align_bytes=64)
-        groups = (
-            {"stream": 0, "first": 0, "bias": bias_prot, "words": prot_words, "scales": prot_scales},
-            {"stream": 0, "first": 2, "bias": bias_prot, "words": prot_words, "scales": prot_scales},
-            {"stream": 1, "first": 0, "bias": bias_mol, "words": mol_words, "scales": mol_scales},
-        )
+        prot_tiles = [
+            {"stream": 0, "t": t, "bias": bias_prot, "words": prot_words, "scales": prot_scales}
+            for t in range(M_PROT // P)
+        ]
+        mol_tiles = [
+            {"stream": 1, "t": t, "bias": bias_mol, "words": mol_words, "scales": mol_scales}
+            for t in range(N_MOL // P)
+        ]
 
-        def add_bias_and_square(group):
-            group["v"] = []
-            sum_sq = finish_pool.tile([P, 2], F32, tag="sum_sq")
-            for a in range(2):
-                v = finish_pool.tile([P, D], F32, tag="v")
-                nc.vector.tensor_tensor(
-                    out=v[:], in0=acc[group["stream"]][group["first"] + a][:], in1=group["bias"][:], op=ALU.add
+        def add_bias(tile):
+            v = finish_pool.tile([P, D], F32, tag="v")
+            nc.vector.tensor_tensor(
+                out=v[:], in0=acc[tile["stream"]][tile["t"]][:], in1=tile["bias"][:], op=ALU.add
+            )
+            tile["v"] = v
+
+        def square_and_root(tile):
+            squares = finish_pool.tile([P, D], BF16, tag="squares")
+            sum_sq = finish_pool.tile([P, 1], F32, tag="sum_sq")
+            nc.scalar.activation(out=squares[:], in_=tile["v"][:], func=ACT.Square, accum_out=sum_sq[:])
+            norm = finish_pool.tile([P, 1], F32, tag="norm")
+            nc.scalar.sqrt(out=norm[:], in_=sum_sq[:])
+            tile["norm"] = norm
+
+        def scale_to_unit(tile):
+            clamped = finish_pool.tile([P, 1], F32, tag="clamped")
+            nc.vector.tensor_scalar_max(out=clamped[:], in0=tile["norm"][:], scalar1=EPS)
+            inv_norm = finish_pool.tile([P, 1], F32, tag="inv_norm")
+            nc.vector.reciprocal(out=inv_norm[:], in_=clamped[:])
+            unit = finish_pool.tile([P, D], BF16, tag="unit")
+            nc.vector.tensor_scalar_mul(out=unit[:], in0=tile["v"][:], scalar1=inv_norm[:])
+            tile["unit"] = unit
+
+        def transpose_unit(tile):
+            unit_grouped = finish_pool.tile([P, P * PACK], BF16, tag="unit_grouped", align_bytes=64)
+            bank = turn_tile([P, PACK, P], BF16)
+            for t in range(PACK):
+                nc.tensor.transpose(
+                    out=bank[:, t, :], in_=tile["unit"][:, t * P : (t + 1) * P], identity=ident_bf16[:]
                 )
-                group["v"].append(v)
-            for a in range(2):
-                squares = finish_pool.tile([P, D], BF16, tag="squares")
-                nc.scalar.activation(
-                    out=squares[:], in_=group["v"][a][:], func=ACT.Square, accum_out=sum_sq[:, a : a + 1]
-                )
-            group["sum_sq"] = sum_sq
+            nc.scalar.copy(
+                out=unit_grouped[:].rearrange("p (r t) -> p r t", t=PACK), in_=bank[:].rearrange("p t r -> p r t")
+            )
+            tile["unit_grouped"] = unit_grouped
 
-        def clamp_and_root(group):
-            clamped = finish_pool.tile([P, 2], F32, tag="clamped")
-            nc.vector.tensor_scalar_max(out=clamped[:], in0=group["sum_sq"][:], scalar1=EPS * EPS)
-            norm = finish_pool.tile([P, 2], F32, tag="norm")
-            nc.scalar.sqrt(out=norm[:], in_=clamped[:])
-            group["norm"] = norm
-
-        def scale_to_unit(group):
-            inv_norm = finish_pool.tile([P, 2], F32, tag="inv_norm")
-            nc.vector.reciprocal(out=inv_norm[:], in_=group["norm"][:])
-            group["unit"] = []
-            for a in range(2):
-                unit = finish_pool.tile([P, D], BF16, tag="unit")
-                nc.vector.tensor_scalar_mul(out=unit[:], in0=group["v"][a][:], scalar1=inv_norm[:, a : a + 1])
-                group["unit"].append(unit)
-
-        def transpose_unit(group):
-            unit_grouped = finish_pool.tile([P, GROUP * PACK], BF16, tag="unit_grouped", align_bytes=64)
-            for a in range(2):
-                bank = turn_tile([P, PACK, P], BF16)
-                for t in range(PACK):
-                    nc.tensor.transpose(
-                        out=bank[:, t, :], in_=group["unit"][a][:, t * P : (t + 1) * P], identity=ident_bf16[:]
-                    )
-                turned = bank[:].rearrange("p t r -> p r t")
-                side_by_side = unit_grouped[:, a * K_PASS : (a + 1) * K_PASS].rearrange("p (r t) -> p r t", t=PACK)
-                if a == 0:
-                    nc.scalar.copy(out=side_by_side, in_=turned)
-                else:
-                    nc.vector.tensor_copy(out=side_by_side, in_=turned)
-            group["unit_grouped"] = unit_grouped
-
-        def quantise_unit(group):
-            cols = slice(group["first"] * P, group["first"] * P + GROUP)
+        def quantise_unit(tile):
+            cols = slice(tile["t"] * P, (tile["t"] + 1) * P)
             nc.vector.quantize_mx(
-                out=group["words"][:, cols].bitcast(FP8X4),
-                scales=group["scales"][:, cols],
-                in_=group["unit_grouped"][:],
+                out=tile["words"][:, cols].bitcast(FP8X4), scales=tile["scales"][:, cols], in_=tile["unit_grouped"][:]
             )
 
-        finish_stages = (add_bias_and_square, clamp_and_root, scale_to_unit, transpose_unit, quantise_unit)
+        def finish_step(step, stages):
+            for s, stage in stages:
+                if 0 <= step - s < len(prot_tiles):
+                    stage(prot_tiles[step - s])
 
-        for i in range(n_rounds + 1):
-            if i >= 1:
-                quantise_round(i - 1)
-            if i < n_rounds:
-                transpose_round(i)
+        with tc.manual_schedule():
+            for i in range(n_rounds):
+                if i >= 1:
+                    quantise_round(i - 1)
+                open_round(i)
+                for a, name in enumerate(("w", "h")):
+                    step = 2 * (i - ROUNDS - 1) + a
+                    transpose_operand(i, name)
+                    finish_step(step, ((2, transpose_unit),))
+                    if i >= 1:
+                        multiply_pass(i - 1, a)
+                    finish_step(step, ((3, quantise_unit), (1, scale_to_unit), (0, square_and_root)))
+                if i == 0:
+                    spread_constants()
                 if i + load_ahead < n_rounds:
                     load_round(i + load_ahead)
-            if i == 0:
-                spread_constants()
-            if i >= 1:
-                multiply_round(i - 1)
-            if i == ROUNDS:
-                add_bias_and_square(groups[0])
-                add_bias_and_square(groups[1])
-                turn_banks.extend((2, 3))
-            step = i - ROUNDS - 1
-            if 0 <= step < 4:
-                for stage in (clamp_and_root, scale_to_unit) if step % 2 == 0 else (transpose_unit, quantise_unit):
-                    stage(groups[step // 2])
-        for stage in finish_stages:
-            stage(groups[2])
+                if i == ROUNDS:
+                    for tile in prot_tiles:
+                        add_bias(tile)
+                    turn_banks.extend((2, 3))
+            quantise_round(n_rounds - 1)
+            for t, tile in enumerate(mol_tiles):
+                for a in range(ROUND):
+                    multiply_tile(n_rounds - 1, a, t)
+                add_bias(tile)
+                square_and_root(tile)
+            for tile in mol_tiles:
+                scale_to_unit(tile)
+                transpose_unit(tile)
+            for tile in mol_tiles:
+                quantise_unit(tile)
 
-        for i in range(M_PROT // P):
-            distance = turn_tile([P, N_MOL], F32)
-            nc.tensor.matmul_mx(
-                out=distance[:],
-                lhsT=prot_words[:, i * P : (i + 1) * P].bitcast(FP8X4),
-                lhsT_scale=prot_scales[:, i * P : (i + 1) * P],
-                rhs=mol_words[:].bitcast(FP8X4),
-                rhs_scale=mol_scales[:],
-                start=True,
-                stop=True,
-            )
-            result = finish_pool.tile([P, N_MOL], F32, tag="result")
-            if i % 2 == 0:
-                nc.scalar.activation(out=result[:], in_=distance[:], func=ACT.Copy, scale=inv_temperature[:, 0:1])
-            else:
-                nc.vector.tensor_scalar_mul(out=result[:], in0=distance[:], scalar1=inv_temperature[:, 0:1])
-            nc.sync.dma_start(out=out[i * P : (i + 1) * P, :], in_=result[:])
+            for tile in mol_tiles:
+                cols = slice(tile["t"] * P, (tile["t"] + 1) * P)
+                for pair in range(M_PROT // (2 * P)):
+                    distance = turn_tile([P, 2, P], F32)
+                    for b in range(2):
+                        i = 2 * pair + b
+                        nc.tensor.matmul_mx(
+                            out=distance[:, b, :],
+                            lhsT=prot_words[:, i * P : (i + 1) * P].bitcast(FP8X4),
+                            lhsT_scale=prot_scales[:, i * P : (i + 1) * P],
+                            rhs=mol_words[:, cols].bitcast(FP8X4),
+                            rhs_scale=mol_scales[:, cols],
+                            start=True,
+                            stop=True,
+                        )
+                    result = finish_pool.tile([P, 2, P], F32, tag="result")
+                    if pair == 0:
+                        nc.scalar.activation(
+                            out=result[:], in_=distance[:], func=ACT.Copy, scale=inv_temperature[:, 0:1]
+                        )
+                    else:
+                        nc.vector.tensor_scalar_mul(out=result[:], in0=distance[:], scalar1=inv_temperature[:, 0:1])
+                    nc.sync.dma_start(
+                        out=out[2 * pair * P : 2 * (pair + 1) * P, cols].rearrange("(b p) c -> p b c", p=P),
+                        in_=result[:],
+                    )

@@ -19,12 +19,15 @@ P = 128
 PACK = 4
 K_PASS = P * PACK
 PASSES = F // K_PASS
-WORDS = K_PASS // 2
 W_TILES = D // P
-ROUND = 2
-ROUND_K = ROUND * K_PASS
-ROUNDS = PASSES // ROUND
-RAW_BUFS = 48
+PROT_TILES = M_PROT // P
+MOL_TILES = N_MOL // P
+LAST = PROT_TILES - 1
+PAIR = 2
+PAIR_K = PAIR * K_PASS
+LAST_PASSES = 8
+RAW_BUFS = 42
+RUN = 4
 TEMP_COLS = 32
 
 
@@ -38,40 +41,51 @@ def tile_coembedding_pa_k_kernel(tc, h_mol, h_prot, Wm2, bm2, Wp2, bp2, temperat
         finish_pool = ctx.enter_context(tc.tile_pool(name="finish", bufs=4))
         psum = ctx.enter_context(tc.psum_pool(name="psum", bufs=1))
 
-        streams = (
-            {"h": h_prot, "w": Wp2, "h_tiles": M_PROT // P},
-            {"h": h_mol, "w": Wm2, "h_tiles": N_MOL // P},
-        )
-        n_rounds = len(streams) * ROUNDS
+        prot = {"w": Wp2, "h": h_prot, "keep": True, "tiles": list(range(LAST))}
+        mol = {"w": Wm2, "h": h_mol, "keep": False, "tiles": list(range(MOL_TILES))}
+        last = {"w": None, "h": h_prot, "keep": False, "tiles": [LAST]}
+        rounds = [(prot, g, PAIR) for g in range(0, PASSES, PAIR)]
+        rounds += [(mol, g, PAIR) for g in range(0, PASSES, PAIR)]
+        rounds += [(last, g, LAST_PASSES) for g in range(0, PASSES, LAST_PASSES)]
+        prot_rounds = mol_rounds = PASSES // PAIR
+
+        def banks_of(r):
+            stream, first, count = rounds[r]
+            banks = []
+            for g in range(first, first + count, PAIR):
+                if stream["w"] is not None:
+                    banks += [("w", t, t, g) for t in range(W_TILES)]
+                banks += [("h", place, t, g) for place, t in enumerate(stream["tiles"])]
+            return banks
 
         def psum_tile(bank, shape, dtype):
             bank_tile = psum.tile(shape, dtype, tag="bank%d" % bank)
             return bank_tile
 
-        turn_banks = [4, 5, 6, 7]
-        turned_so_far = []
+        acc_bank = {("prot", 0): 0, ("prot", 1): 1, ("prot", 2): 2, ("mol", 0): 0, ("mol", 1): 1, ("prot", LAST): 2}
+        turn_banks = (3, 4, 5, 6, 7)
+        turned = []
 
         def turn_tile(shape, dtype):
-            bank = turn_banks[len(turned_so_far) % len(turn_banks)]
-            turned_so_far.append(bank)
+            bank = turn_banks[len(turned) % len(turn_banks)]
+            turned.append(bank)
             return psum_tile(bank, shape, dtype)
 
+        loads = [(r, bank) for r in range(len(rounds)) for bank in banks_of(r)]
         raw = {}
 
-        def load_round(r):
-            stream = streams[r // ROUNDS]
-            k_first = (r % ROUNDS) * ROUND_K
-            for name, matrix, tiles in (("w", stream["w"], W_TILES), ("h", stream["h"], stream["h_tiles"])):
-                for t in range(tiles):
-                    rows_tile = raw_pool.tile([P, ROUND_K], BF16, tag="rows")
-                    nc.sync.dma_start(
-                        out=rows_tile[:], in_=matrix[t * P : (t + 1) * P, k_first : k_first + ROUND_K]
-                    )
-                    raw[(r, name, t)] = rows_tile
+        def load_until(count):
+            while len(raw) < min(count, len(loads)):
+                r, bank = loads[len(raw)]
+                operand, place, t, g = bank
+                matrix = rounds[r][0][operand]
+                raw_tile = raw_pool.tile([P, PAIR_K], BF16, tag="raw")
+                nc.sync.dma_start(
+                    out=raw_tile[:], in_=matrix[t * P : (t + 1) * P, g * K_PASS : g * K_PASS + PAIR_K]
+                )
+                raw[(r, bank)] = raw_tile
 
-        load_ahead = RAW_BUFS // (W_TILES + M_PROT // P)
-        for r in range(load_ahead):
-            load_round(r)
+        load_until(RAW_BUFS)
 
         ident_f32 = const.tile([P, P], F32)
         make_identity(nc, ident_f32[:])
@@ -102,94 +116,100 @@ def tile_coembedding_pa_k_kernel(tc, h_mol, h_prot, Wm2, bm2, Wp2, bp2, temperat
             nc.tensor.matmul(out=spread_t[:], lhsT=ones[:], rhs=rows[:, 2 * D :], start=True, stop=True)
             nc.vector.reciprocal(out=inv_temperature[:], in_=spread_t[:, 0:1])
 
+        kept_words = const.tile([P, PASSES * D], U32, align_bytes=64)
+        kept_scales = const.tile([P, PASSES * D], U8, align_bytes=64)
         grouped = {}
         codes = {}
         acc = {}
 
         def open_round(r):
-            stream = streams[r // ROUNDS]
-            w_grouped = grouped_pool.tile([P, ROUND * D * PACK], BF16, tag="w_grouped", align_bytes=64)
-            h_grouped = grouped_pool.tile([P, ROUND * stream["h_tiles"] * P * PACK], BF16, tag="h_grouped", align_bytes=64)
-            grouped[r] = (w_grouped, h_grouped)
+            stream, first, count = rounds[r]
+            h_grouped = grouped_pool.tile([P, count * len(stream["tiles"]) * P * PACK], BF16, tag="h_grouped", align_bytes=64)
+            grouped[r] = {"h": h_grouped}
+            if stream["w"] is not None:
+                w_grouped = grouped_pool.tile([P, count * D * PACK], BF16, tag="w_grouped", align_bytes=64)
+                grouped[r]["w"] = w_grouped
 
-        def transpose_operand(r, name):
-            tiles = W_TILES if name == "w" else streams[r // ROUNDS]["h_tiles"]
-            target = grouped[r][0 if name == "w" else 1]
-            for t in range(tiles):
-                words = raw[(r, name, t)][:].bitcast(F32)
-                bank = turn_tile([P, 2 * ROUND, P], F32)
-                for block in range(2 * ROUND):
-                    nc.tensor.transpose(
-                        out=bank[:, block, :], in_=words[:, block * P : (block + 1) * P], identity=ident_f32[:]
-                    )
-                turned = bank[:].rearrange("p (a u) r -> p a r u", u=2)
-                side_by_side = target[:].bitcast(F32).rearrange("p (a t r u) -> p a t r u", a=ROUND, t=tiles, u=2)
-                side_by_side = side_by_side[:, :, t]
-                if (name, t) in (("w", 2), ("h", 0), ("h", 2)):
-                    nc.vector.tensor_copy(out=side_by_side, in_=turned)
-                else:
-                    nc.scalar.copy(out=side_by_side, in_=turned)
+        def transpose_bank(r, index, bank):
+            stream, first, count = rounds[r]
+            operand, place, t, g = bank
+            tiles = W_TILES if operand == "w" else len(stream["tiles"])
+            words = raw[(r, bank)][:].bitcast(F32)
+            blocks = turn_tile([P, 2 * PAIR, P], F32)
+            for block in range(2 * PAIR):
+                nc.tensor.transpose(
+                    out=blocks[:, block, :], in_=words[:, block * P : (block + 1) * P], identity=ident_f32[:]
+                )
+            halves = blocks[:].rearrange("p (a u) r -> p a r u", u=2)
+            side_by_side = grouped[r][operand][:].bitcast(F32).rearrange("p (a t r u) -> p a t r u", a=count, t=tiles, u=2)
+            side_by_side = side_by_side[:, g - first : g - first + PAIR, place]
+            if index % 3 == 1:
+                nc.vector.tensor_copy(out=side_by_side, in_=halves)
+            else:
+                nc.scalar.copy(out=side_by_side, in_=halves)
 
         def quantise_round(r):
-            h_cols = streams[r // ROUNDS]["h_tiles"] * P
-            w_grouped, h_grouped = grouped[r]
-            w_words = codes_pool.tile([P, ROUND * D], U32, tag="w_words", align_bytes=64)
-            w_scales = codes_pool.tile([P, ROUND * D], U8, tag="w_scales", align_bytes=64)
-            h_words = codes_pool.tile([P, ROUND * h_cols], U32, tag="h_words", align_bytes=64)
-            h_scales = codes_pool.tile([P, ROUND * h_cols], U8, tag="h_scales", align_bytes=64)
-            for a in range(ROUND):
-                for words, scales, source, cols in (
-                    (w_words, w_scales, w_grouped, D),
-                    (h_words, h_scales, h_grouped, h_cols),
-                ):
-                    nc.vector.quantize_mx(
-                        out=words[:, a * cols : (a + 1) * cols].bitcast(FP8X4),
-                        scales=scales[:, a * cols : (a + 1) * cols],
-                        in_=source[:, a * cols * PACK : (a + 1) * cols * PACK],
+            stream, first, count = rounds[r]
+            h_cols = len(stream["tiles"]) * P
+            h_words = codes_pool.tile([P, count * h_cols], U32, tag="h_words", align_bytes=64)
+            h_scales = codes_pool.tile([P, count * h_cols], U8, tag="h_scales", align_bytes=64)
+            operands = {"h": (h_words, h_scales, 0, h_cols)}
+            if stream["w"] is None or stream["keep"]:
+                operands["w"] = (kept_words, kept_scales, first * D, D)
+            else:
+                w_words = codes_pool.tile([P, count * D], U32, tag="w_words", align_bytes=64)
+                w_scales = codes_pool.tile([P, count * D], U8, tag="w_scales", align_bytes=64)
+                operands["w"] = (w_words, w_scales, 0, D)
+            for a in range(count):
+                for operand in ("w", "h"):
+                    if operand in grouped[r]:
+                        words, scales, start, cols = operands[operand]
+                        for piece, width in ((0, 2 * P), (2 * P, P)) if cols == 3 * P else ((0, cols),):
+                            at = slice(start + a * cols + piece, start + a * cols + piece + width)
+                            k_at = slice((a * cols + piece) * PACK, (a * cols + piece + width) * PACK)
+                            nc.vector.quantize_mx(
+                                out=words[:, at].bitcast(FP8X4),
+                                scales=scales[:, at],
+                                in_=grouped[r][operand][:, k_at],
+                            )
+            codes[r] = operands
+
+        def multiply(r, passes):
+            stream, first, count = rounds[r]
+            h_words, h_scales, h_start, h_cols = codes[r]["h"]
+            w_words, w_scales, w_start, w_cols = codes[r]["w"]
+            name = "mol" if stream is mol else "prot"
+            for a in passes:
+                for place, t in enumerate(stream["tiles"]):
+                    if first + a == 0:
+                        acc_tile = psum_tile(acc_bank[(name, t)], [P, D], F32)
+                        acc[(name, t)] = acc_tile
+                    h_at = slice(a * h_cols + place * P, a * h_cols + (place + 1) * P)
+                    w_at = slice(w_start + a * D, w_start + (a + 1) * D)
+                    nc.tensor.matmul_mx(
+                        out=acc[(name, t)][:],
+                        lhsT=h_words[:, h_at].bitcast(FP8X4),
+                        lhsT_scale=h_scales[:, h_at],
+                        rhs=w_words[:, w_at].bitcast(FP8X4),
+                        rhs_scale=w_scales[:, w_at],
+                        start=(first + a == 0),
+                        stop=(first + a == PASSES - 1),
                     )
-            codes[r] = (w_words, w_scales, h_words, h_scales)
-
-        def multiply_tile(r, a, i):
-            number = r // ROUNDS
-            h_cols = streams[number]["h_tiles"] * P
-            acc_tiles = acc.setdefault(number, [])
-            if i == len(acc_tiles):
-                acc_tile = psum_tile(i, [P, D], F32)
-                acc_tiles.append(acc_tile)
-            w_words, w_scales, h_words, h_scales = codes[r]
-            h_first = a * h_cols + i * P
-            nc.tensor.matmul_mx(
-                out=acc_tiles[i][:],
-                lhsT=h_words[:, h_first : h_first + P].bitcast(FP8X4),
-                lhsT_scale=h_scales[:, h_first : h_first + P],
-                rhs=w_words[:, a * D : (a + 1) * D].bitcast(FP8X4),
-                rhs_scale=w_scales[:, a * D : (a + 1) * D],
-                start=(r % ROUNDS == 0 and a == 0),
-                stop=(r % ROUNDS == ROUNDS - 1 and a == ROUND - 1),
-            )
-
-        def multiply_pass(r, a):
-            for i in range(streams[r // ROUNDS]["h_tiles"]):
-                multiply_tile(r, a, i)
 
         prot_words = const.tile([P, M_PROT], U32, align_bytes=64)
         prot_scales = const.tile([P, M_PROT], U8, align_bytes=64)
         mol_words = const.tile([P, N_MOL], U32, align_bytes=64)
         mol_scales = const.tile([P, N_MOL], U8, align_bytes=64)
         prot_tiles = [
-            {"stream": 0, "t": t, "bias": bias_prot, "words": prot_words, "scales": prot_scales}
-            for t in range(M_PROT // P)
+            {"acc": ("prot", t), "bias": bias_prot, "words": prot_words, "scales": prot_scales} for t in range(PROT_TILES)
         ]
         mol_tiles = [
-            {"stream": 1, "t": t, "bias": bias_mol, "words": mol_words, "scales": mol_scales}
-            for t in range(N_MOL // P)
+            {"acc": ("mol", t), "bias": bias_mol, "words": mol_words, "scales": mol_scales} for t in range(MOL_TILES)
         ]
 
         def add_bias(tile):
             v = finish_pool.tile([P, D], F32, tag="v")
-            nc.vector.tensor_tensor(
-                out=v[:], in0=acc[tile["stream"]][tile["t"]][:], in1=tile["bias"][:], op=ALU.add
-            )
+            nc.vector.tensor_tensor(out=v[:], in0=acc[tile["acc"]][:], in1=tile["bias"][:], op=ALU.add)
             tile["v"] = v
 
         def square_and_root(tile):
@@ -209,84 +229,88 @@ def tile_coembedding_pa_k_kernel(tc, h_mol, h_prot, Wm2, bm2, Wp2, bp2, temperat
             nc.vector.tensor_scalar_mul(out=unit[:], in0=tile["v"][:], scalar1=inv_norm[:])
             tile["unit"] = unit
 
-        def transpose_unit(tile):
+        def transpose_unit(tile, copy):
             unit_grouped = finish_pool.tile([P, P * PACK], BF16, tag="unit_grouped", align_bytes=64)
-            bank = turn_tile([P, PACK, P], BF16)
+            blocks = turn_tile([P, PACK, P], BF16)
             for t in range(PACK):
                 nc.tensor.transpose(
-                    out=bank[:, t, :], in_=tile["unit"][:, t * P : (t + 1) * P], identity=ident_bf16[:]
+                    out=blocks[:, t, :], in_=tile["unit"][:, t * P : (t + 1) * P], identity=ident_bf16[:]
                 )
-            nc.scalar.copy(
-                out=unit_grouped[:].rearrange("p (r t) -> p r t", t=PACK), in_=bank[:].rearrange("p t r -> p r t")
-            )
+            copy(out=unit_grouped[:].rearrange("p (r t) -> p r t", t=PACK), in_=blocks[:].rearrange("p t r -> p r t"))
             tile["unit_grouped"] = unit_grouped
 
         def quantise_unit(tile):
-            cols = slice(tile["t"] * P, (tile["t"] + 1) * P)
+            first = tile["acc"][1] * P
             nc.vector.quantize_mx(
-                out=tile["words"][:, cols].bitcast(FP8X4), scales=tile["scales"][:, cols], in_=tile["unit_grouped"][:]
+                out=tile["words"][:, first : first + P].bitcast(FP8X4),
+                scales=tile["scales"][:, first : first + P],
+                in_=tile["unit_grouped"][:],
             )
+
+        def turn_beside_rounds(tile):
+            transpose_unit(tile, nc.scalar.copy)
 
         def finish_step(step, stages):
             for s, stage in stages:
-                if 0 <= step - s < len(prot_tiles):
+                if 0 <= step - s < LAST:
                     stage(prot_tiles[step - s])
 
+        consumed = []
         with tc.manual_schedule():
-            for i in range(n_rounds):
-                if i >= 1:
-                    quantise_round(i - 1)
-                open_round(i)
-                for a, name in enumerate(("w", "h")):
-                    step = 2 * (i - ROUNDS - 1) + a
-                    transpose_operand(i, name)
-                    finish_step(step, ((2, transpose_unit),))
-                    if i >= 1:
-                        multiply_pass(i - 1, a)
+            for r in range(len(rounds)):
+                if r >= 1:
+                    quantise_round(r - 1)
+                open_round(r)
+                banks = banks_of(r)
+                passes = list(range(rounds[r - 1][2])) if r >= 1 else []
+                runs = (banks[:RUN], banks[RUN:]) if len(banks) > RUN else (banks,)
+                for n, run in enumerate(runs):
+                    step = 2 * (r - prot_rounds - 1) + n
+                    for bank in run:
+                        transpose_bank(r, len(consumed), bank)
+                        consumed.append(bank)
+                    finish_step(step, ((2, turn_beside_rounds),))
+                    if r >= 1:
+                        multiply(r - 1, passes[n * len(passes) // len(runs) : (n + 1) * len(passes) // len(runs)])
                     finish_step(step, ((3, quantise_unit), (1, scale_to_unit), (0, square_and_root)))
-                if i == 0:
+                if r == 0:
                     spread_constants()
-                if i + load_ahead < n_rounds:
-                    load_round(i + load_ahead)
-                if i == ROUNDS:
-                    for tile in prot_tiles:
+                load_until(len(consumed) + RAW_BUFS)
+                if r == prot_rounds:
+                    for tile in prot_tiles[:LAST]:
                         add_bias(tile)
-                    turn_banks.extend((2, 3))
-            quantise_round(n_rounds - 1)
-            for t, tile in enumerate(mol_tiles):
-                for a in range(ROUND):
-                    multiply_tile(n_rounds - 1, a, t)
-                add_bias(tile)
-                square_and_root(tile)
+                if r == prot_rounds + mol_rounds:
+                    for tile in mol_tiles:
+                        add_bias(tile)
+                        square_and_root(tile)
+            r = len(rounds) - 1
+            quantise_round(r)
+            multiply(r, list(range(rounds[r][2])))
             for tile in mol_tiles:
                 scale_to_unit(tile)
-                transpose_unit(tile)
+            add_bias(prot_tiles[LAST])
+            square_and_root(prot_tiles[LAST])
             for tile in mol_tiles:
+                transpose_unit(tile, nc.vector.tensor_copy)
+            scale_to_unit(prot_tiles[LAST])
+            transpose_unit(prot_tiles[LAST], nc.scalar.copy)
+            for tile in mol_tiles + prot_tiles[LAST:]:
                 quantise_unit(tile)
 
-            for tile in mol_tiles:
-                cols = slice(tile["t"] * P, (tile["t"] + 1) * P)
-                for pair in range(M_PROT // (2 * P)):
-                    distance = turn_tile([P, 2, P], F32)
-                    for b in range(2):
-                        i = 2 * pair + b
-                        nc.tensor.matmul_mx(
-                            out=distance[:, b, :],
-                            lhsT=prot_words[:, i * P : (i + 1) * P].bitcast(FP8X4),
-                            lhsT_scale=prot_scales[:, i * P : (i + 1) * P],
-                            rhs=mol_words[:, cols].bitcast(FP8X4),
-                            rhs_scale=mol_scales[:, cols],
-                            start=True,
-                            stop=True,
-                        )
-                    result = finish_pool.tile([P, 2, P], F32, tag="result")
-                    if pair == 0:
-                        nc.scalar.activation(
-                            out=result[:], in_=distance[:], func=ACT.Copy, scale=inv_temperature[:, 0:1]
-                        )
-                    else:
-                        nc.vector.tensor_scalar_mul(out=result[:], in0=distance[:], scalar1=inv_temperature[:, 0:1])
-                    nc.sync.dma_start(
-                        out=out[2 * pair * P : 2 * (pair + 1) * P, cols].rearrange("(b p) c -> p b c", p=P),
-                        in_=result[:],
-                    )
+            for t in range(PROT_TILES):
+                distance = turn_tile([P, N_MOL], F32)
+                nc.tensor.matmul_mx(
+                    out=distance[:],
+                    lhsT=prot_words[:, t * P : (t + 1) * P].bitcast(FP8X4),
+                    lhsT_scale=prot_scales[:, t * P : (t + 1) * P],
+                    rhs=mol_words[:].bitcast(FP8X4),
+                    rhs_scale=mol_scales[:],
+                    start=True,
+                    stop=True,
+                )
+                result = finish_pool.tile([P, N_MOL], F32, tag="result")
+                if t % 2 == 0:
+                    nc.scalar.activation(out=result[:], in_=distance[:], func=ACT.Copy, scale=inv_temperature[:, 0:1])
+                else:
+                    nc.vector.tensor_scalar_mul(out=result[:], in0=distance[:], scalar1=inv_temperature[:, 0:1])
+                nc.sync.dma_start(out=out[t * P : (t + 1) * P, :], in_=result[:])

@@ -28,6 +28,7 @@ PAIR_K = PAIR * K_PASS
 LAST_PASSES = 8
 RAW_BUFS = 42
 RUN = 4
+HEAD_MATMULS = 4
 TEMP_COLS = 32
 
 
@@ -87,6 +88,8 @@ def tile_coembedding_pa_k_kernel(tc, h_mol, h_prot, Wm2, bm2, Wp2, bp2, temperat
 
         load_until(RAW_BUFS)
 
+        zeros = const.tile([P, D], BF16)
+        nc.vector.memset(zeros[:], 0.0)
         ident_f32 = const.tile([P, P], F32)
         make_identity(nc, ident_f32[:])
         ident_bf16 = const.tile([P, P], BF16)
@@ -255,8 +258,14 @@ def tile_coembedding_pa_k_kernel(tc, h_mol, h_prot, Wm2, bm2, Wp2, bp2, temperat
                 if 0 <= step - s < LAST:
                     stage(prot_tiles[step - s])
 
+        def keep_clock(tile, count):
+            for n in range(count):
+                nc.tensor.matmul(out=tile[:], lhsT=zeros[:, 0:P], rhs=zeros[:], start=True, stop=True)
+
         consumed = []
         with tc.manual_schedule():
+            unread = psum_tile(0, [P, D], F32)
+            keep_clock(unread, HEAD_MATMULS)
             for r in range(len(rounds)):
                 if r >= 1:
                     quantise_round(r - 1)
@@ -269,6 +278,8 @@ def tile_coembedding_pa_k_kernel(tc, h_mol, h_prot, Wm2, bm2, Wp2, bp2, temperat
                     for bank in run:
                         transpose_bank(r, len(consumed), bank)
                         consumed.append(bank)
+                        if r == 0:
+                            keep_clock(unread, 1)
                     finish_step(step, ((2, turn_beside_rounds),))
                     if r >= 1:
                         multiply(r - 1, passes[n * len(passes) // len(runs) : (n + 1) * len(passes) // len(runs)])

@@ -63,14 +63,19 @@ def tile_coembedding_pa_k_kernel(tc, h_mol, h_prot, Wm2, bm2, Wp2, bp2, temperat
             bank_tile = psum.tile(shape, dtype, tag="bank%d" % bank)
             return bank_tile
 
-        acc_bank = {("prot", 0): 0, ("prot", 1): 1, ("prot", 2): 2, ("mol", 0): 0, ("mol", 1): 1, ("prot", LAST): 2}
-        turn_banks = (3, 4, 5, 6, 7)
+        acc_bank = {("prot", 0): 0, ("prot", 1): 1, ("prot", 2): 2, ("mol", 0): 6, ("mol", 1): 7, ("prot", LAST): 2}
+        turn_banks = [3, 4, 5, 6, 7]
         turned = []
 
         def turn_tile(shape, dtype):
             bank = turn_banks[len(turned) % len(turn_banks)]
             turned.append(bank)
             return psum_tile(bank, shape, dtype)
+
+        def turn_in(banks):
+            turn_banks.clear()
+            turn_banks.extend(banks)
+            turned.clear()
 
         loads = [(r, bank) for r in range(len(rounds)) for bank in banks_of(r)]
         raw = {}
@@ -133,7 +138,7 @@ def tile_coembedding_pa_k_kernel(tc, h_mol, h_prot, Wm2, bm2, Wp2, bp2, temperat
                 w_grouped = grouped_pool.tile([P, count * D * PACK], BF16, tag="w_grouped", align_bytes=64)
                 grouped[r]["w"] = w_grouped
 
-        def transpose_bank(r, index, bank):
+        def transpose_bank(r, bank, is_last):
             stream, first, count = rounds[r]
             operand, place, t, g = bank
             tiles = W_TILES if operand == "w" else len(stream["tiles"])
@@ -146,12 +151,12 @@ def tile_coembedding_pa_k_kernel(tc, h_mol, h_prot, Wm2, bm2, Wp2, bp2, temperat
             halves = blocks[:].rearrange("p (a u) r -> p a r u", u=2)
             side_by_side = grouped[r][operand][:].bitcast(F32).rearrange("p (a t r u) -> p a t r u", a=count, t=tiles, u=2)
             side_by_side = side_by_side[:, g - first : g - first + PAIR, place]
-            if index % 3 == 1:
+            if is_last:
                 nc.vector.tensor_copy(out=side_by_side, in_=halves)
             else:
                 nc.scalar.copy(out=side_by_side, in_=halves)
 
-        def quantise_round(r):
+        def quantise_round(r, tiles_to_add=()):
             stream, first, count = rounds[r]
             h_cols = len(stream["tiles"]) * P
             h_words = codes_pool.tile([P, count * h_cols], U32, tag="h_words", align_bytes=64)
@@ -175,6 +180,9 @@ def tile_coembedding_pa_k_kernel(tc, h_mol, h_prot, Wm2, bm2, Wp2, bp2, temperat
                                 scales=scales[:, at],
                                 in_=grouped[r][operand][:, k_at],
                             )
+                if a == 0:
+                    for tile in tiles_to_add:
+                        add_bias(tile)
             codes[r] = operands
 
         def multiply(r, passes):
@@ -267,8 +275,10 @@ def tile_coembedding_pa_k_kernel(tc, h_mol, h_prot, Wm2, bm2, Wp2, bp2, temperat
             unread = psum_tile(0, [P, D], F32)
             keep_clock(unread, HEAD_MATMULS)
             for r in range(len(rounds)):
+                if r == prot_rounds + 1:
+                    turn_in((3, 4, 5, 0, 1))
                 if r >= 1:
-                    quantise_round(r - 1)
+                    quantise_round(r - 1, prot_tiles[:LAST] if r == prot_rounds + 1 else ())
                 open_round(r)
                 banks = banks_of(r)
                 passes = list(range(rounds[r - 1][2])) if r >= 1 else []
@@ -276,7 +286,7 @@ def tile_coembedding_pa_k_kernel(tc, h_mol, h_prot, Wm2, bm2, Wp2, bp2, temperat
                 for n, run in enumerate(runs):
                     step = 2 * (r - prot_rounds - 1) + n
                     for bank in run:
-                        transpose_bank(r, len(consumed), bank)
+                        transpose_bank(r, bank, bank == banks[-1])
                         consumed.append(bank)
                         if r == 0:
                             keep_clock(unread, 1)
@@ -287,9 +297,6 @@ def tile_coembedding_pa_k_kernel(tc, h_mol, h_prot, Wm2, bm2, Wp2, bp2, temperat
                 if r == 0:
                     spread_constants()
                 load_until(len(consumed) + RAW_BUFS)
-                if r == prot_rounds:
-                    for tile in prot_tiles[:LAST]:
-                        add_bias(tile)
                 if r == prot_rounds + mol_rounds:
                     for tile in mol_tiles:
                         add_bias(tile)

@@ -27,8 +27,11 @@ PAIR = 2
 PAIR_K = PAIR * K_PASS
 LAST_PASSES = 8
 RAW_BUFS = 42
+BLOCKS = 2 * PAIR
+COLD_ROUNDS = 1
 RUN = 4
 HEAD_MATMULS = 4
+TAIL_MATMULS = 4
 TEMP_COLS = 32
 
 
@@ -63,19 +66,15 @@ def tile_coembedding_pa_k_kernel(tc, h_mol, h_prot, Wm2, bm2, Wp2, bp2, temperat
             bank_tile = psum.tile(shape, dtype, tag="bank%d" % bank)
             return bank_tile
 
-        acc_bank = {("prot", 0): 0, ("prot", 1): 1, ("prot", 2): 2, ("mol", 0): 6, ("mol", 1): 7, ("prot", LAST): 2}
-        turn_banks = [3, 4, 5, 6, 7]
+        acc_banks = {("prot", 0): (0,), ("prot", 1): (1,), ("prot", 2): (2,), ("mol", 0): (0,), ("mol", 1): (1,)}
+        acc_banks[("prot", LAST)] = (2, 0)
+        turn_banks = (3, 4, 5, 6, 7)
         turned = []
 
         def turn_tile(shape, dtype):
             bank = turn_banks[len(turned) % len(turn_banks)]
             turned.append(bank)
             return psum_tile(bank, shape, dtype)
-
-        def turn_in(banks):
-            turn_banks.clear()
-            turn_banks.extend(banks)
-            turned.clear()
 
         loads = [(r, bank) for r in range(len(rounds)) for bank in banks_of(r)]
         raw = {}
@@ -138,16 +137,16 @@ def tile_coembedding_pa_k_kernel(tc, h_mol, h_prot, Wm2, bm2, Wp2, bp2, temperat
                 w_grouped = grouped_pool.tile([P, count * D * PACK], BF16, tag="w_grouped", align_bytes=64)
                 grouped[r]["w"] = w_grouped
 
-        def transpose_bank(r, bank, is_last):
+        def transpose_block(r, bank, blocks, block):
+            words = raw[(r, bank)][:].bitcast(F32)
+            nc.tensor.transpose(
+                out=blocks[:, block, :], in_=words[:, block * P : (block + 1) * P], identity=ident_f32[:]
+            )
+
+        def empty_bank(r, bank, blocks, is_last):
             stream, first, count = rounds[r]
             operand, place, t, g = bank
             tiles = W_TILES if operand == "w" else len(stream["tiles"])
-            words = raw[(r, bank)][:].bitcast(F32)
-            blocks = turn_tile([P, 2 * PAIR, P], F32)
-            for block in range(2 * PAIR):
-                nc.tensor.transpose(
-                    out=blocks[:, block, :], in_=words[:, block * P : (block + 1) * P], identity=ident_f32[:]
-                )
             halves = blocks[:].rearrange("p (a u) r -> p a r u", u=2)
             side_by_side = grouped[r][operand][:].bitcast(F32).rearrange("p (a t r u) -> p a t r u", a=count, t=tiles, u=2)
             side_by_side = side_by_side[:, g - first : g - first + PAIR, place]
@@ -156,7 +155,7 @@ def tile_coembedding_pa_k_kernel(tc, h_mol, h_prot, Wm2, bm2, Wp2, bp2, temperat
             else:
                 nc.scalar.copy(out=side_by_side, in_=halves)
 
-        def quantise_round(r, tiles_to_add=()):
+        def quantise_round(r):
             stream, first, count = rounds[r]
             h_cols = len(stream["tiles"]) * P
             h_words = codes_pool.tile([P, count * h_cols], U32, tag="h_words", align_bytes=64)
@@ -180,25 +179,27 @@ def tile_coembedding_pa_k_kernel(tc, h_mol, h_prot, Wm2, bm2, Wp2, bp2, temperat
                                 scales=scales[:, at],
                                 in_=grouped[r][operand][:, k_at],
                             )
-                if a == 0:
-                    for tile in tiles_to_add:
-                        add_bias(tile)
             codes[r] = operands
 
-        def multiply(r, passes):
+        def multiply(r, a, place, parts=(0, 1)):
             stream, first, count = rounds[r]
             h_words, h_scales, h_start, h_cols = codes[r]["h"]
             w_words, w_scales, w_start, w_cols = codes[r]["w"]
             name = "mol" if stream is mol else "prot"
-            for a in passes:
-                for place, t in enumerate(stream["tiles"]):
-                    if first + a == 0:
-                        acc_tile = psum_tile(acc_bank[(name, t)], [P, D], F32)
-                        acc[(name, t)] = acc_tile
-                    h_at = slice(a * h_cols + place * P, a * h_cols + (place + 1) * P)
-                    w_at = slice(w_start + a * D, w_start + (a + 1) * D)
+            t = stream["tiles"][place]
+            if first + a == 0 and (name, t) not in acc:
+                acc[(name, t)] = []
+                width = D // len(acc_banks[(name, t)])
+                for part, bank in enumerate(acc_banks[(name, t)]):
+                    acc_tile = psum_tile(bank, [P, width], F32)
+                    acc[(name, t)].append((acc_tile, slice(part * width, (part + 1) * width)))
+            h_at = slice(a * h_cols + place * P, a * h_cols + (place + 1) * P)
+            for part, (acc_tile, features) in enumerate(acc[(name, t)]):
+                if part in parts:
+                    w_first = w_start + a * D
+                    w_at = slice(w_first + features.start, w_first + features.stop)
                     nc.tensor.matmul_mx(
-                        out=acc[(name, t)][:],
+                        out=acc_tile[:],
                         lhsT=h_words[:, h_at].bitcast(FP8X4),
                         lhsT_scale=h_scales[:, h_at],
                         rhs=w_words[:, w_at].bitcast(FP8X4),
@@ -220,15 +221,24 @@ def tile_coembedding_pa_k_kernel(tc, h_mol, h_prot, Wm2, bm2, Wp2, bp2, temperat
 
         def add_bias(tile):
             v = finish_pool.tile([P, D], F32, tag="v")
-            nc.vector.tensor_tensor(out=v[:], in0=acc[tile["acc"]][:], in1=tile["bias"][:], op=ALU.add)
+            for acc_tile, features in acc[tile["acc"]]:
+                nc.vector.tensor_tensor(
+                    out=v[:, features], in0=acc_tile[:], in1=tile["bias"][:, features], op=ALU.add
+                )
             tile["v"] = v
 
         def square_and_root(tile):
             squares = finish_pool.tile([P, D], BF16, tag="squares")
-            sum_sq = finish_pool.tile([P, 1], F32, tag="sum_sq")
-            nc.scalar.activation(out=squares[:], in_=tile["v"][:], func=ACT.Square, accum_out=sum_sq[:])
+            sums = []
+            for acc_tile, features in acc[tile["acc"]]:
+                sum_sq = finish_pool.tile([P, 1], F32, tag="sum_sq")
+                nc.scalar.activation(
+                    out=squares[:, features], in_=tile["v"][:, features], func=ACT.Square, accum_out=sum_sq[:]
+                )
+                sums.append(sum_sq)
             norm = finish_pool.tile([P, 1], F32, tag="norm")
-            nc.scalar.sqrt(out=norm[:], in_=sum_sq[:])
+            other = sums[1][:] if len(sums) == 2 else 0.0
+            nc.scalar.activation(out=norm[:], in_=sums[0][:], func=ACT.Sqrt, bias=other)
             tile["norm"] = norm
 
         def scale_to_unit(tile):
@@ -237,7 +247,13 @@ def tile_coembedding_pa_k_kernel(tc, h_mol, h_prot, Wm2, bm2, Wp2, bp2, temperat
             inv_norm = finish_pool.tile([P, 1], F32, tag="inv_norm")
             nc.vector.reciprocal(out=inv_norm[:], in_=clamped[:])
             unit = finish_pool.tile([P, D], BF16, tag="unit")
-            nc.vector.tensor_scalar_mul(out=unit[:], in0=tile["v"][:], scalar1=inv_norm[:])
+            for part, (acc_tile, features) in enumerate(acc[tile["acc"]]):
+                if part == 0:
+                    nc.vector.tensor_scalar_mul(out=unit[:, features], in0=tile["v"][:, features], scalar1=inv_norm[:])
+                else:
+                    nc.scalar.activation(
+                        out=unit[:, features], in_=tile["v"][:, features], func=ACT.Copy, scale=inv_norm[:]
+                    )
             tile["unit"] = unit
 
         def transpose_unit(tile, copy):
@@ -271,45 +287,77 @@ def tile_coembedding_pa_k_kernel(tc, h_mol, h_prot, Wm2, bm2, Wp2, bp2, temperat
                 nc.tensor.matmul(out=tile[:], lhsT=zeros[:, 0:P], rhs=zeros[:], start=True, stop=True)
 
         consumed = []
+        multiplied = {"prot": [], "mol": []}
+
+        def multiply_due(name, stream, its_rounds):
+            first_bank = sum(len(banks_of(r)) for r in range(its_rounds[0]))
+            per_round = len(banks_of(its_rounds[0]))
+            behind = len(consumed) - first_bank - RUN
+            passes = [
+                (r, a, place) for r in its_rounds for a in range(rounds[r][2]) for place in range(len(stream["tiles"]))
+            ]
+            mx_per_round = len(passes) // len(its_rounds)
+            available = mx_per_round * max(0, behind // per_round)
+            count = min(available, mx_per_round * max(0, behind - RUN) // per_round)
+            if available >= len(passes):
+                count = len(passes)
+            while len(multiplied[name]) < count:
+                item = passes[len(multiplied[name])]
+                multiply(*item)
+                multiplied[name].append(item)
+            return count == len(passes)
+
+        prot_list = list(range(prot_rounds))
+        mol_list = list(range(prot_rounds, prot_rounds + mol_rounds))
+        closed = []
         with tc.manual_schedule():
             unread = psum_tile(0, [P, D], F32)
             keep_clock(unread, HEAD_MATMULS)
             for r in range(len(rounds)):
-                if r == prot_rounds + 1:
-                    turn_in((3, 4, 5, 0, 1))
                 if r >= 1:
-                    quantise_round(r - 1, prot_tiles[:LAST] if r == prot_rounds + 1 else ())
+                    quantise_round(r - 1)
                 open_round(r)
                 banks = banks_of(r)
-                passes = list(range(rounds[r - 1][2])) if r >= 1 else []
-                runs = (banks[:RUN], banks[RUN:]) if len(banks) > RUN else (banks,)
-                for n, run in enumerate(runs):
-                    step = 2 * (r - prot_rounds - 1) + n
-                    for bank in run:
-                        transpose_bank(r, bank, bank == banks[-1])
-                        consumed.append(bank)
-                        if r == 0:
-                            keep_clock(unread, 1)
-                    finish_step(step, ((2, turn_beside_rounds),))
-                    if r >= 1:
-                        multiply(r - 1, passes[n * len(passes) // len(runs) : (n + 1) * len(passes) // len(runs)])
-                    finish_step(step, ((3, quantise_unit), (1, scale_to_unit), (0, square_and_root)))
+                for n, bank in enumerate(banks):
+                    blocks = turn_tile([P, BLOCKS, P], F32)
+                    for block in range(BLOCKS):
+                        transpose_block(r, bank, blocks, block)
+                    empty_bank(r, bank, blocks, n == len(banks) - 1)
+                    if r < COLD_ROUNDS:
+                        keep_clock(unread, 1)
+                    consumed.append(bank)
+                    if len(consumed) % RUN == 0:
+                        step = len(closed) - 1
+                        finish_step(step, ((2, turn_beside_rounds),))
+                        if multiply_due("prot", prot, prot_list):
+                            if not closed:
+                                for tile in prot_tiles[:LAST]:
+                                    add_bias(tile)
+                            closed.append(r)
+                        if multiply_due("mol", mol, mol_list) and r == len(rounds) - 2:
+                            for tile in mol_tiles:
+                                add_bias(tile)
+                                square_and_root(tile)
+                        if r == len(rounds) - 1:
+                            for a in range(LAST_PASSES):
+                                multiply(r - 1, a, 0)
+                        finish_step(step, ((3, quantise_unit), (1, scale_to_unit), (0, square_and_root)))
                 if r == 0:
                     spread_constants()
                 load_until(len(consumed) + RAW_BUFS)
-                if r == prot_rounds + mol_rounds:
-                    for tile in mol_tiles:
-                        add_bias(tile)
-                        square_and_root(tile)
             r = len(rounds) - 1
             quantise_round(r)
-            multiply(r, list(range(rounds[r][2])))
+            for part in range(2):
+                for a in range(rounds[r][2]):
+                    multiply(r, a, 0, (part,))
             for tile in mol_tiles:
                 scale_to_unit(tile)
             add_bias(prot_tiles[LAST])
             square_and_root(prot_tiles[LAST])
             for tile in mol_tiles:
                 transpose_unit(tile, nc.vector.tensor_copy)
+            unread = turn_tile([P, D], F32)
+            keep_clock(unread, TAIL_MATMULS)
             scale_to_unit(prot_tiles[LAST])
             transpose_unit(prot_tiles[LAST], nc.scalar.copy)
             for tile in mol_tiles + prot_tiles[LAST:]:

@@ -28,8 +28,10 @@ PAIR_K = PAIR * K_PASS
 LAST_PASSES = 8
 RAW_BUFS = 42
 BLOCKS = 2 * PAIR
-COLD_ROUNDS = 1
 RUN = 4
+MOL_RUN = 3
+LAG = 4
+SPREAD = 5
 HEAD_MATMULS = 4
 TAIL_MATMULS = 4
 TEMP_COLS = 32
@@ -66,15 +68,20 @@ def tile_coembedding_pa_k_kernel(tc, h_mol, h_prot, Wm2, bm2, Wp2, bp2, temperat
             bank_tile = psum.tile(shape, dtype, tag="bank%d" % bank)
             return bank_tile
 
-        acc_banks = {("prot", 0): (0,), ("prot", 1): (1,), ("prot", 2): (2,), ("mol", 0): (0,), ("mol", 1): (1,)}
-        acc_banks[("prot", LAST)] = (2, 0)
-        turn_banks = (3, 4, 5, 6, 7)
+        acc_banks = {("prot", 0): (0,), ("prot", 1): (1,), ("prot", 2): (2,), ("mol", 0): (6,), ("mol", 1): (7,)}
+        acc_banks[("prot", LAST)] = (2, 6)
+        turn_banks = [3, 4, 5, 6, 7]
         turned = []
 
         def turn_tile(shape, dtype):
             bank = turn_banks[len(turned) % len(turn_banks)]
             turned.append(bank)
             return psum_tile(bank, shape, dtype)
+
+        def turn_in(banks):
+            turn_banks.clear()
+            turn_banks.extend(banks)
+            turned.clear()
 
         loads = [(r, bank) for r in range(len(rounds)) for bank in banks_of(r)]
         raw = {}
@@ -96,8 +103,6 @@ def tile_coembedding_pa_k_kernel(tc, h_mol, h_prot, Wm2, bm2, Wp2, bp2, temperat
         nc.vector.memset(zeros[:], 0.0)
         ident_f32 = const.tile([P, P], F32)
         make_identity(nc, ident_f32[:])
-        ident_bf16 = const.tile([P, P], BF16)
-        make_identity(nc, ident_bf16[:])
         ones = const.tile([P, P], BF16)
         nc.vector.memset(ones[:], 1.0)
         rows = const.tile([P, 2 * D + TEMP_COLS], BF16)
@@ -258,12 +263,14 @@ def tile_coembedding_pa_k_kernel(tc, h_mol, h_prot, Wm2, bm2, Wp2, bp2, temperat
 
         def transpose_unit(tile, copy):
             unit_grouped = finish_pool.tile([P, P * PACK], BF16, tag="unit_grouped", align_bytes=64)
-            blocks = turn_tile([P, PACK, P], BF16)
-            for t in range(PACK):
-                nc.tensor.transpose(
-                    out=blocks[:, t, :], in_=tile["unit"][:, t * P : (t + 1) * P], identity=ident_bf16[:]
-                )
-            copy(out=unit_grouped[:].rearrange("p (r t) -> p r t", t=PACK), in_=blocks[:].rearrange("p t r -> p r t"))
+            words = tile["unit"][:].bitcast(F32)
+            blocks = turn_tile([P, 2, P], F32)
+            for u in range(2):
+                nc.tensor.transpose(out=blocks[:, u, :], in_=words[:, u * P : (u + 1) * P], identity=ident_f32[:])
+            copy(
+                out=unit_grouped[:].bitcast(F32).rearrange("p (r u) -> p r u", u=2),
+                in_=blocks[:].rearrange("p u r -> p r u"),
+            )
             tile["unit_grouped"] = unit_grouped
 
         def quantise_unit(tile):
@@ -289,17 +296,17 @@ def tile_coembedding_pa_k_kernel(tc, h_mol, h_prot, Wm2, bm2, Wp2, bp2, temperat
         consumed = []
         multiplied = {"prot": [], "mol": []}
 
-        def multiply_due(name, stream, its_rounds):
+        def multiply_due(name, stream, its_rounds, close):
             first_bank = sum(len(banks_of(r)) for r in range(its_rounds[0]))
             per_round = len(banks_of(its_rounds[0]))
-            behind = len(consumed) - first_bank - RUN
+            behind = len(consumed) - first_bank - LAG
             passes = [
                 (r, a, place) for r in its_rounds for a in range(rounds[r][2]) for place in range(len(stream["tiles"]))
             ]
             mx_per_round = len(passes) // len(its_rounds)
             available = mx_per_round * max(0, behind // per_round)
-            count = min(available, mx_per_round * max(0, behind - RUN) // per_round)
-            if available >= len(passes):
+            count = min(available, mx_per_round * max(0, behind - SPREAD) // per_round, len(passes))
+            if close:
                 count = len(passes)
             while len(multiplied[name]) < count:
                 item = passes[len(multiplied[name])]
@@ -310,12 +317,17 @@ def tile_coembedding_pa_k_kernel(tc, h_mol, h_prot, Wm2, bm2, Wp2, bp2, temperat
         prot_list = list(range(prot_rounds))
         mol_list = list(range(prot_rounds, prot_rounds + mol_rounds))
         closed = []
+        in_run = []
         with tc.manual_schedule():
             unread = psum_tile(0, [P, D], F32)
             keep_clock(unread, HEAD_MATMULS)
             for r in range(len(rounds)):
                 if r >= 1:
                     quantise_round(r - 1)
+                if r == prot_rounds + 1:
+                    turn_in((3, 4, 5))
+                if r == prot_rounds + 2:
+                    turn_in((3, 4, 5, 0, 1))
                 open_round(r)
                 banks = banks_of(r)
                 for n, bank in enumerate(banks):
@@ -323,18 +335,21 @@ def tile_coembedding_pa_k_kernel(tc, h_mol, h_prot, Wm2, bm2, Wp2, bp2, temperat
                     for block in range(BLOCKS):
                         transpose_block(r, bank, blocks, block)
                     empty_bank(r, bank, blocks, n == len(banks) - 1)
-                    if r < COLD_ROUNDS:
+                    if not multiplied["prot"]:
                         keep_clock(unread, 1)
                     consumed.append(bank)
-                    if len(consumed) % RUN == 0:
+                    in_run.append(bank)
+                    if len(in_run) == (MOL_RUN if rounds[r][0] is mol else RUN):
+                        in_run.clear()
                         step = len(closed) - 1
                         finish_step(step, ((2, turn_beside_rounds),))
-                        if multiply_due("prot", prot, prot_list):
+                        if multiply_due("prot", prot, prot_list, False):
                             if not closed:
                                 for tile in prot_tiles[:LAST]:
                                     add_bias(tile)
                             closed.append(r)
-                        if multiply_due("mol", mol, mol_list) and r == len(rounds) - 2:
+                        multiply_due("mol", mol, mol_list, r == len(rounds) - 2)
+                        if r == len(rounds) - 2:
                             for tile in mol_tiles:
                                 add_bias(tile)
                                 square_and_root(tile)

from contextlib import ExitStack

import concourse.mybir as mybir
from concourse.masks import make_identity

F32 = mybir.dt.float32
BF16 = mybir.dt.bfloat16
U32 = mybir.dt.uint32
U8 = mybir.dt.uint8
FP8X4 = mybir.dt.float8_e4m3fn_x4
ALU = mybir.AluOpType
ACT = mybir.ActivationFunctionType

N_MOL, M_PROT, F, D = 256, 512, 8192, 512
EPS = 1e-8
FLOPS = 2 * F * D * (N_MOL + M_PROT) + 2 * M_PROT * N_MOL * D

P = 128
PACK = 4
K_PASS = P * PACK
PASSES = F // K_PASS
W_TILES = D // P
PROT_TILES = M_PROT // P
MOL_TILES = N_MOL // P
LAST = PROT_TILES - 1
PAIR = 2
PAIR_K = PAIR * K_PASS
LAST_PASSES = 8
RAW_BUFS = 42
BLOCKS = 2 * PAIR
RUN = 4
MOL_RUN = 3
LAG = 4
SPREAD = 5
HEAD_MATMULS = 4
TAIL_MATMULS = 4
TEMP_COLS = 32


def tile_coembedding_pa_k_kernel(tc, h_mol, h_prot, Wm2, bm2, Wp2, bp2, temperature, out):
    nc = tc.nc
    with ExitStack() as ctx:
        const = ctx.enter_context(tc.tile_pool(name="const", bufs=1))
        raw_pool = ctx.enter_context(tc.tile_pool(name="raw", bufs=RAW_BUFS))
        grouped_pool = ctx.enter_context(tc.tile_pool(name="grouped", bufs=2))
        codes_pool = ctx.enter_context(tc.tile_pool(name="codes", bufs=2))
        finish_pool = ctx.enter_context(tc.tile_pool(name="finish", bufs=4))
        psum = ctx.enter_context(tc.psum_pool(name="psum", bufs=1))

        prot = {"w": Wp2, "h": h_prot, "keep": True, "tiles": list(range(LAST))}
        mol = {"w": Wm2, "h": h_mol, "keep": False, "tiles": list(range(MOL_TILES))}
        last = {"w": None, "h": h_prot, "keep": False, "tiles": [LAST]}
        rounds = [(prot, g, PAIR) for g in range(0, PASSES, PAIR)]
        rounds += [(mol, g, PAIR) for g in range(0, PASSES, PAIR)]
        rounds += [(last, g, LAST_PASSES) for g in range(0, PASSES, LAST_PASSES)]
        prot_rounds = mol_rounds = PASSES // PAIR

        def banks_of(r):
            stream, first, count = rounds[r]
            banks = []
            for g in range(first, first + count, PAIR):
                if stream["w"] is not None:
                    banks += [("w", t, t, g) for t in range(W_TILES)]
                banks += [("h", place, t, g) for place, t in enumerate(stream["tiles"])]
            return banks

        def psum_tile(bank, shape, dtype):
            bank_tile = psum.tile(shape, dtype, tag="bank%d" % bank)
            return bank_tile

        acc_banks = {("prot", 0): (0,), ("prot", 1): (1,), ("prot", 2): (2,), ("mol", 0): (6,), ("mol", 1): (7,)}
        acc_banks[("prot", LAST)] = (2, 6)
        turn_banks = [3, 4, 5, 6, 7]
        turned = []

        def turn_tile(shape, dtype):
            bank = turn_banks[len(turned) % len(turn_banks)]
            turned.append(bank)
            return psum_tile(bank, shape, dtype)

        def turn_in(banks):
            turn_banks.clear()
            turn_banks.extend(banks)
            turned.clear()

        loads = [(r, bank) for r in range(len(rounds)) for bank in banks_of(r)]
        raw = {}

        def load_until(count):
            while len(raw) < min(count, len(loads)):
                r, bank = loads[len(raw)]
                operand, place, t, g = bank
                matrix = rounds[r][0][operand]
                raw_tile = raw_pool.tile([P, PAIR_K], BF16, tag="raw")
                nc.sync.dma_start(
                    out=raw_tile[:], in_=matrix[t * P : (t + 1) * P, g * K_PASS : g * K_PASS + PAIR_K]
                )
                raw[(r, bank)] = raw_tile

        load_until(RAW_BUFS)

        zeros = const.tile([P, D], BF16)
        nc.vector.memset(zeros[:], 0.0)
        ident_f32 = const.tile([P, P], F32)
        make_identity(nc, ident_f32[:])
        ones = const.tile([P, P], BF16)
        nc.vector.memset(ones[:], 1.0)
        rows = const.tile([P, 2 * D + TEMP_COLS], BF16)
        nc.vector.memset(rows[:], 0.0)
        nc.scalar.dma_start(out=rows[0:1, 0:D], in_=bp2.rearrange("(o d) -> o d", o=1))
        nc.scalar.dma_start(out=rows[0:1, D : 2 * D], in_=bm2.rearrange("(o d) -> o d", o=1))
        nc.scalar.dma_start(out=rows[0:1, 2 * D : 2 * D + 1], in_=temperature.rearrange("(o d) -> o d", o=1))
        one = const.tile([P, 1], F32)
        nc.vector.memset(one[:], 1.0)
        root_of_one = const.tile([P, 1], F32)
        nc.scalar.sqrt(out=root_of_one[:], in_=one[:])

        bias_prot = const.tile([P, D], F32)
        bias_mol = const.tile([P, D], F32)
        inv_temperature = const.tile([P, 1], F32)

        def spread_constants():
            for bias, first in ((bias_prot, 0), (bias_mol, D)):
                spread = turn_tile([P, D], F32)
                nc.tensor.matmul(out=spread[:], lhsT=ones[:], rhs=rows[:, first : first + D], start=True, stop=True)
                nc.vector.tensor_copy(out=bias[:], in_=spread[:])
            spread_t = turn_tile([P, TEMP_COLS], F32)
            nc.tensor.matmul(out=spread_t[:], lhsT=ones[:], rhs=rows[:, 2 * D :], start=True, stop=True)
            nc.vector.reciprocal(out=inv_temperature[:], in_=spread_t[:, 0:1])

        kept_words = const.tile([P, PASSES * D], U32, align_bytes=64)
        kept_scales = const.tile([P, PASSES * D], U8, align_bytes=64)
        grouped = {}
        codes = {}
        acc = {}

        def open_round(r):
            stream, first, count = rounds[r]
            h_grouped = grouped_pool.tile([P, count * len(stream["tiles"]) * P * PACK], BF16, tag="h_grouped", align_bytes=64)
            grouped[r] = {"h": h_grouped}
            if stream["w"] is not None:
                w_grouped = grouped_pool.tile([P, count * D * PACK], BF16, tag="w_grouped", align_bytes=64)
                grouped[r]["w"] = w_grouped

        def transpose_block(r, bank, blocks, block):
            words = raw[(r, bank)][:].bitcast(F32)
            nc.tensor.transpose(
                out=blocks[:, block, :], in_=words[:, block * P : (block + 1) * P], identity=ident_f32[:]
            )

        def empty_bank(r, bank, blocks, is_last):
            stream, first, count = rounds[r]
            operand, place, t, g = bank
            tiles = W_TILES if operand == "w" else len(stream["tiles"])
            halves = blocks[:].rearrange("p (a u) r -> p a r u", u=2)
            side_by_side = grouped[r][operand][:].bitcast(F32).rearrange("p (a t r u) -> p a t r u", a=count, t=tiles, u=2)
            side_by_side = side_by_side[:, g - first : g - first + PAIR, place]
            if is_last:
                nc.vector.tensor_copy(out=side_by_side, in_=halves)
            else:
                nc.scalar.copy(out=side_by_side, in_=halves)

        def quantise_round(r):
            stream, first, count = rounds[r]
            h_cols = len(stream["tiles"]) * P
            h_words = codes_pool.tile([P, count * h_cols], U32, tag="h_words", align_bytes=64)
            h_scales = codes_pool.tile([P, count * h_cols], U8, tag="h_scales", align_bytes=64)
            operands = {"h": (h_words, h_scales, 0, h_cols)}
            if stream["w"] is None or stream["keep"]:
                operands["w"] = (kept_words, kept_scales, first * D, D)
            else:
                w_words = codes_pool.tile([P, count * D], U32, tag="w_words", align_bytes=64)
                w_scales = codes_pool.tile([P, count * D], U8, tag="w_scales", align_bytes=64)
                operands["w"] = (w_words, w_scales, 0, D)
            for a in range(count):
                for operand in ("w", "h"):
                    if operand in grouped[r]:
                        words, scales, start, cols = operands[operand]
                        for piece, width in ((0, 2 * P), (2 * P, P)) if cols == 3 * P else ((0, cols),):
                            at = slice(start + a * cols + piece, start + a * cols + piece + width)
                            k_at = slice((a * cols + piece) * PACK, (a * cols + piece + width) * PACK)
                            nc.vector.quantize_mx(
                                out=words[:, at].bitcast(FP8X4),
                                scales=scales[:, at],
                                in_=grouped[r][operand][:, k_at],
                            )
            codes[r] = operands

        def multiply(r, a, place, parts=(0, 1)):
            stream, first, count = rounds[r]
            h_words, h_scales, h_start, h_cols = codes[r]["h"]
            w_words, w_scales, w_start, w_cols = codes[r]["w"]
            name = "mol" if stream is mol else "prot"
            t = stream["tiles"][place]
            if first + a == 0 and (name, t) not in acc:
                acc[(name, t)] = []
                width = D // len(acc_banks[(name, t)])
                for part, bank in enumerate(acc_banks[(name, t)]):
                    acc_tile = psum_tile(bank, [P, width], F32)
                    acc[(name, t)].append((acc_tile, slice(part * width, (part + 1) * width)))
            h_at = slice(a * h_cols + place * P, a * h_cols + (place + 1) * P)
            for part, (acc_tile, features) in enumerate(acc[(name, t)]):
                if part in parts:
                    w_first = w_start + a * D
                    w_at = slice(w_first + features.start, w_first + features.stop)
                    nc.tensor.matmul_mx(
                        out=acc_tile[:],
                        lhsT=h_words[:, h_at].bitcast(FP8X4),
                        lhsT_scale=h_scales[:, h_at],
                        rhs=w_words[:, w_at].bitcast(FP8X4),
                        rhs_scale=w_scales[:, w_at],
                        start=(first + a == 0),
                        stop=(first + a == PASSES - 1),
                    )

        prot_words = const.tile([P, M_PROT], U32, align_bytes=64)
        prot_scales = const.tile([P, M_PROT], U8, align_bytes=64)
        mol_words = const.tile([P, N_MOL], U32, align_bytes=64)
        mol_scales = const.tile([P, N_MOL], U8, align_bytes=64)
        prot_tiles = [
            {"acc": ("prot", t), "bias": bias_prot, "words": prot_words, "scales": prot_scales} for t in range(PROT_TILES)
        ]
        mol_tiles = [
            {"acc": ("mol", t), "bias": bias_mol, "words": mol_words, "scales": mol_scales} for t in range(MOL_TILES)
        ]

        def add_bias(tile):
            v = finish_pool.tile([P, D], F32, tag="v")
            for acc_tile, features in acc[tile["acc"]]:
                nc.vector.tensor_tensor(
                    out=v[:, features], in0=acc_tile[:], in1=tile["bias"][:, features], op=ALU.add
                )
            tile["v"] = v

        def square_and_root(tile):
            squares = finish_pool.tile([P, D], BF16, tag="squares")
            sums = []
            for acc_tile, features in acc[tile["acc"]]:
                sum_sq = finish_pool.tile([P, 1], F32, tag="sum_sq")
                nc.scalar.activation(
                    out=squares[:, features], in_=tile["v"][:, features], func=ACT.Square, accum_out=sum_sq[:]
                )
                sums.append(sum_sq)
            norm = finish_pool.tile([P, 1], F32, tag="norm")
            other = sums[1][:] if len(sums) == 2 else 0.0
            nc.scalar.activation(out=norm[:], in_=sums[0][:], func=ACT.Sqrt, bias=other)
            tile["norm"] = norm

        def scale_to_unit(tile):
            clamped = finish_pool.tile([P, 1], F32, tag="clamped")
            nc.vector.tensor_scalar_max(out=clamped[:], in0=tile["norm"][:], scalar1=EPS)
            inv_norm = finish_pool.tile([P, 1], F32, tag="inv_norm")
            nc.vector.reciprocal(out=inv_norm[:], in_=clamped[:])
            unit = finish_pool.tile([P, D], BF16, tag="unit")
            for part, (acc_tile, features) in enumerate(acc[tile["acc"]]):
                if part == 0:
                    nc.vector.tensor_scalar_mul(out=unit[:, features], in0=tile["v"][:, features], scalar1=inv_norm[:])
                else:
                    nc.scalar.activation(
                        out=unit[:, features], in_=tile["v"][:, features], func=ACT.Copy, scale=inv_norm[:]
                    )
            tile["unit"] = unit

        def transpose_unit(tile, copy):
            unit_grouped = finish_pool.tile([P, P * PACK], BF16, tag="unit_grouped", align_bytes=64)
            words = tile["unit"][:].bitcast(F32)
            blocks = turn_tile([P, 2, P], F32)
            for u in range(2):
                nc.tensor.transpose(out=blocks[:, u, :], in_=words[:, u * P : (u + 1) * P], identity=ident_f32[:])
            copy(
                out=unit_grouped[:].bitcast(F32).rearrange("p (r u) -> p r u", u=2),
                in_=blocks[:].rearrange("p u r -> p r u"),
            )
            tile["unit_grouped"] = unit_grouped

        def quantise_unit(tile):
            first = tile["acc"][1] * P
            nc.vector.quantize_mx(
                out=tile["words"][:, first : first + P].bitcast(FP8X4),
                scales=tile["scales"][:, first : first + P],
                in_=tile["unit_grouped"][:],
            )

        def turn_beside_rounds(tile):
            transpose_unit(tile, nc.scalar.copy)

        def finish_step(step, stages):
            for s, stage in stages:
                if 0 <= step - s < LAST:
                    stage(prot_tiles[step - s])

        def keep_clock(tile, count):
            for n in range(count):
                nc.tensor.matmul(out=tile[:], lhsT=zeros[:, 0:P], rhs=zeros[:], start=True, stop=True)

        consumed = []
        multiplied = {"prot": [], "mol": []}

        def multiply_due(name, stream, its_rounds, close):
            first_bank = sum(len(banks_of(r)) for r in range(its_rounds[0]))
            per_round = len(banks_of(its_rounds[0]))
            behind = len(consumed) - first_bank - LAG
            passes = [
                (r, a, place) for r in its_rounds for a in range(rounds[r][2]) for place in range(len(stream["tiles"]))
            ]
            mx_per_round = len(passes) // len(its_rounds)
            available = mx_per_round * max(0, behind // per_round)
            count = min(available, mx_per_round * max(0, behind - SPREAD) // per_round, len(passes))
            if close:
                count = len(passes)
            while len(multiplied[name]) < count:
                item = passes[len(multiplied[name])]
                multiply(*item)
                multiplied[name].append(item)
            return count == len(passes)

        prot_list = list(range(prot_rounds))
        mol_list = list(range(prot_rounds, prot_rounds + mol_rounds))
        closed = []
        in_run = []
        with tc.manual_schedule():
            unread = psum_tile(0, [P, D], F32)
            keep_clock(unread, HEAD_MATMULS)
            for r in range(len(rounds)):
                if r >= 1:
                    quantise_round(r - 1)
                if r == prot_rounds + 1:
                    turn_in((3, 4, 5))
                if r == prot_rounds + 2:
                    turn_in((3, 4, 5, 0, 1))
                open_round(r)
                banks = banks_of(r)
                for n, bank in enumerate(banks):
                    blocks = turn_tile([P, BLOCKS, P], F32)
                    for block in range(BLOCKS):
                        transpose_block(r, bank, blocks, block)
                    empty_bank(r, bank, blocks, n == len(banks) - 1)
                    if not multiplied["prot"]:
                        keep_clock(unread, 1)
                    consumed.append(bank)
                    in_run.append(bank)
                    if len(in_run) == (MOL_RUN if rounds[r][0] is mol else RUN):
                        in_run.clear()
                        step = len(closed) - 1
                        finish_step(step, ((2, turn_beside_rounds),))
                        if multiply_due("prot", prot, prot_list, False):
                            if not closed:
                                for tile in prot_tiles[:LAST]:
                                    add_bias(tile)
                            closed.append(r)
                        multiply_due("mol", mol, mol_list, r == len(rounds) - 2)
                        if r == len(rounds) - 2:
                            for tile in mol_tiles:
                                add_bias(tile)
                                square_and_root(tile)
                        if r == len(rounds) - 1:
                            for a in range(LAST_PASSES):
                                multiply(r - 1, a, 0)
                        finish_step(step, ((3, quantise_unit), (1, scale_to_unit), (0, square_and_root)))
                if r == 0:
                    spread_constants()
                load_until(len(consumed) + RAW_BUFS)
            r = len(rounds) - 1
            quantise_round(r)
            for part in range(2):
                for a in range(rounds[r][2]):
                    multiply(r, a, 0, (part,))
            for tile in mol_tiles:
                scale_to_unit(tile)
            add_bias(prot_tiles[LAST])
            square_and_root(prot_tiles[LAST])
            for tile in mol_tiles:
                transpose_unit(tile, nc.vector.tensor_copy)
            unread = turn_tile([P, D], F32)
            keep_clock(unread, TAIL_MATMULS)
            scale_to_unit(prot_tiles[LAST])
            transpose_unit(prot_tiles[LAST], nc.scalar.copy)
            for tile in mol_tiles + prot_tiles[LAST:]:
                quantise_unit(tile)

            for t in range(PROT_TILES):
                distance = turn_tile([P, N_MOL], F32)
                nc.tensor.matmul_mx(
                    out=distance[:],
                    lhsT=prot_words[:, t * P : (t + 1) * P].bitcast(FP8X4),
                    lhsT_scale=prot_scales[:, t * P : (t + 1) * P],
                    rhs=mol_words[:].bitcast(FP8X4),
                    rhs_scale=mol_scales[:],
                    start=True,
                    stop=True,
                )
                result = finish_pool.tile([P, N_MOL], F32, tag="result")
                if t % 2 == 0:
                    nc.scalar.activation(out=result[:], in_=distance[:], func=ACT.Copy, scale=inv_temperature[:, 0:1])
                else:
                    nc.vector.tensor_scalar_mul(out=result[:], in0=distance[:], scalar1=inv_temperature[:, 0:1])
                nc.sync.dma_start(out=out[t * P : (t + 1) * P, :], in_=result[:])
